import numpy as np
import ml_dtypes

BF16 = ml_dtypes.bfloat16


def bf(x):
    return np.asarray(x, np.float32).astype(BF16)


def f32(x):
    return np.asarray(x, np.float32)


def f64(x):
    return np.asarray(x).astype(np.float64)


def striped(idx):
    return np.tile(idx.reshape(-1, 16).T, (8, 1))


F, C, S, N = 512, 512, 4096, 2048
ALPHA = 0.2
DENS = 0.01


def setup_inputs():
    lim_w = np.sqrt(6.0 / (F + C))
    lim_a = np.sqrt(6.0 / (1 + C))
    x = bf(np.random.standard_normal((F, N)))
    w = bf(np.random.uniform(-lim_w, lim_w, (F, C)))
    attn_src = bf(np.random.uniform(-lim_a, lim_a, (C, 1)))
    attn_dst = bf(np.random.uniform(-lim_a, lim_a, (C, 1)))
    adj_t = f32(np.maximum(np.random.random((N, N)) < DENS, np.eye(N)))
    base = f32(np.random.standard_normal((C, S)))
    return {"x": x, "w": w, "attn_src": attn_src, "attn_dst": attn_dst, "adj_t": adj_t, "base": base, "offs": striped(np.random.permutation(S)[:N])}


def reference(x, w, attn_src, attn_dst, adj_t, base, offs):
    idx = offs[:16].T.reshape(-1)
    h = f64(w).T @ f64(x)
    a_src = f64(attn_src).T @ h
    a_dst = f64(attn_dst).T @ h
    sc = a_src.T + a_dst
    e = f64(adj_t) * np.exp(np.maximum(sc, ALPHA * sc))
    att = e / e.sum(axis=0, keepdims=True)
    v = h @ att
    p = np.maximum(v, 0.0)
    q = np.exp(np.minimum(v, 0.0)) - 1.0
    out = f64(base).copy()
    out[:, idx] = p + q
    return out

@@ -1,0 +1,192 @@
+import concourse.mybir as mybir
+from concourse.masks import make_identity
+
+F32 = mybir.dt.float32
+BF16 = mybir.dt.bfloat16
+U16 = mybir.dt.uint16
+ALU = mybir.AluOpType
+ACT = mybir.ActivationFunctionType
+AXIS_X = mybir.AxisListType.X
+
+P = 128
+F, C, N, SLOTS = 512, 512, 2048, 4096
+SLOPE = 0.2
+BANK = 512
+KB = F // P
+CB = C // P
+UB = N // P
+JC = N // BANK
+UB_PER_PANEL = BANK // P
+
+FLOPS = 2 * F * C * N + 2 * 2 * C * N + 2 * C * N * N
+
+
+def tile_sparsegraphattention_b_kernel(tc, x, w, attn_src, attn_dst, adj_t, base, offs, out):
+    nc = tc.nc
+    with (
+        tc.tile_pool(name="held", bufs=1) as held,
+        tc.tile_pool(name="windows", bufs=2) as windows,
+        tc.psum_pool(name="banks", bufs=8) as banks,
+    ):
+        def bank(name):
+            return banks.tile([P, BANK], F32, tag="bank", name=name)
+
+        def chunk(jc):
+            return slice(jc * BANK, (jc + 1) * BANK)
+
+        def load_window(cb):
+            window = windows.tile([P, SLOTS], F32, name="window")
+            nc.sync.dma_start(window[:], base[cb * P : (cb + 1) * P, :])
+            return window
+
+        offsets = held.tile([P, N // 16], U16, name="offsets")
+        nc.sync.dma_start(offsets[:], offs)
+
+        h_t = [held.tile([P, C], BF16, name=f"h_t{b}") for b in range(UB)]
+        e = [held.tile([P, N], BF16, name=f"e{b}") for b in range(UB)]
+        inv_sum = [held.tile([P, BANK], F32, name=f"inv_sum{jc}") for jc in range(JC)]
+
+        with (
+            tc.tile_pool(name="early", bufs=1) as early,
+            tc.tile_pool(name="scratch", bufs=2) as scratch,
+            tc.tile_pool(name="adjacency", bufs=5) as adjacency,
+            tc.tile_pool(name="second_terms", bufs=3) as second_terms,
+        ):
+            w_sb = early.tile([P, KB, C], BF16, name="w_sb")
+            nc.sync.dma_start(w_sb[:], w.rearrange("(kb p) c -> p kb c", p=P))
+            attn_rows = []
+            for name, vector in (("dst", attn_dst), ("src", attn_src)):
+                row = early.tile([P, C], BF16, name=f"attn_{name}_row")
+                nc.sync.dma_start(row[:], vector.rearrange("c one -> (c one)").partition_broadcast(P))
+                attn_rows.append(row)
+            x_panels = []
+            for jc in range(JC):
+                panel = early.tile([P, KB, BANK], BF16, name=f"x_panel{jc}")
+                nc.sync.dma_start(panel[:], x[:, chunk(jc)].rearrange("(kb p) u -> p kb u", p=P))
+                x_panels.append(panel)
+
+            def x_block(b, kb):
+                first = (b % UB_PER_PANEL) * P
+                return x_panels[b // UB_PER_PANEL][:, kb, first : first + P]
+
+            ones = early.tile([P, P], BF16, name="ones")
+            nc.vector.memset(ones[:], 1.0)
+            identity = early.tile([P, P], F32, name="identity")
+            make_identity(nc, identity[:])
+
+            w_attn = early.tile([P, 2, KB], F32, name="w_attn")
+            for v, row in enumerate(attn_rows):
+                for kb in range(KB):
+                    products = scratch.tile([P, C], F32, name="products")
+                    nc.vector.scalar_tensor_tensor(
+                        out=products[:], in0=w_sb[:, kb, :], scalar=1.0, in1=row[:],
+                        op0=ALU.mult, op1=ALU.mult, accum_out=w_attn[:, v, kb : kb + 1],
+                    )
+            w_dst_cols = early.tile([P, KB, P], BF16, name="w_dst_cols")
+            nc.vector.tensor_copy(w_dst_cols[:], w_attn[:, 0, :].unsqueeze(2).to_broadcast([P, KB, P]))
+            w_src_col = early.tile([P, KB], BF16, name="w_src_col")
+            nc.vector.tensor_copy(w_src_col[:], w_attn[:, 1, :])
+
+            a_dst_rows = early.tile([P, N], F32, name="a_dst_rows")
+            for jc in range(JC):
+                a_dst_ps = bank(f"a_dst_ps{jc}")
+                for kb in range(KB):
+                    nc.tensor.matmul(
+                        a_dst_ps[:], lhsT=w_dst_cols[:, kb, :], rhs=x_panels[jc][:, kb, :],
+                        start=(kb == 0), stop=(kb == KB - 1),
+                    )
+                nc.scalar.copy(a_dst_rows[:, chunk(jc)], a_dst_ps[:])
+
+            a_src_ps = bank("a_src_ps")
+            for b in range(UB):
+                for kb in range(KB):
+                    nc.tensor.matmul(
+                        a_src_ps[:, b : b + 1], lhsT=x_block(b, kb), rhs=w_src_col[:, kb : kb + 1],
+                        start=(kb == 0), stop=(kb == KB - 1),
+                    )
+            a_src = early.tile([P, UB], F32, name="a_src")
+            nc.vector.tensor_copy(a_src[:], a_src_ps[:, 0:UB])
+
+            own_max = early.tile([P, 1], F32, name="own_max")
+            nc.vector.reduce_max(out=own_max[:], in_=a_src[:], axis=AXIS_X)
+            own_max_cols = early.tile([P, P], F32, name="own_max_cols")
+            nc.vector.tensor_copy(own_max_cols[:], own_max[:].to_broadcast([P, P]))
+            maxima_ps = bank("maxima_ps")
+            nc.tensor.matmul(maxima_ps[:, 0:P], lhsT=own_max_cols[:], rhs=identity[:], start=True, stop=True)
+            top = early.tile([P, 1], F32, name="top")
+            nc.vector.reduce_max(out=top[:], in_=maxima_ps[:, 0:P], axis=AXIS_X)
+
+            shifted = early.tile([P, UB], F32, name="shifted")
+            nc.vector.tensor_scalar(
+                out=shifted[:], in0=a_src[:], scalar1=top[:, 0:1], scalar2=None, op0=ALU.subtract
+            )
+            first_term = early.tile([P, UB], F32, name="first_term")
+            nc.scalar.activation(out=first_term[:], in_=shifted[:], func=ACT.Exp)
+            second_bias = early.tile([P, UB], F32, name="second_bias")
+            nc.vector.tensor_scalar(
+                out=second_bias[:], in0=a_src[:], scalar1=SLOPE, scalar2=top[:, 0:1],
+                op0=ALU.mult, op1=ALU.subtract,
+            )
+
+            for b in range(UB):
+                h_ps = bank(f"h_ps{b}")
+                for kb in range(KB):
+                    nc.tensor.matmul(
+                        h_ps[:], lhsT=x_block(b, kb), rhs=w_sb[:, kb, :],
+                        start=(kb == 0), stop=(kb == KB - 1),
+                    )
+                nc.scalar.copy(h_t[b][:], h_ps[:])
+
+            sum_ps = [bank(f"sum_ps{jc}") for jc in range(JC)]
+            for b in range(UB):
+                adj = adjacency.tile([P, N], F32, name="adj")
+                nc.sync.dma_start(adj[:], adj_t[b * P : (b + 1) * P, :])
+                second_term = second_terms.tile([P, N], F32, name="second_term")
+                nc.scalar.activation(
+                    out=second_term[:], in_=a_dst_rows[:], func=ACT.Exp,
+                    bias=second_bias[:, b : b + 1], scale=SLOPE - 1.0,
+                )
+                nc.vector.scalar_tensor_tensor(
+                    out=e[b][:], in0=second_term[:], scalar=first_term[:, b : b + 1], in1=adj[:],
+                    op0=ALU.max, op1=ALU.mult,
+                )
+                for jc in range(JC):
+                    nc.tensor.matmul(
+                        sum_ps[jc][:], lhsT=ones[:], rhs=e[b][:, chunk(jc)],
+                        start=(b == 0), stop=(b == UB - 1),
+                    )
+            next_windows = [load_window(0), load_window(1)]
+
+            for jc in range(JC):
+                nc.scalar.activation(out=inv_sum[jc][:], in_=sum_ps[jc][:], func=ACT.Ln)
+            for jc in range(JC):
+                nc.scalar.activation(out=inv_sum[jc][:], in_=inv_sum[jc][:], func=ACT.Exp, scale=-1.0)
+
+        with (
+            tc.tile_pool(name="addends", bufs=2) as addends,
+            tc.tile_pool(name="chunks", bufs=3) as chunks,
+        ):
+            for cb in range(CB):
+                p = addends.tile([P, N], F32, name="p")
+                q = addends.tile([P, N], F32, name="q")
+                for jc in range(JC):
+                    v_ps = bank(f"v_ps{cb}_{jc}")
+                    for b in range(UB):
+                        nc.tensor.matmul(
+                            v_ps[:], lhsT=h_t[b][:, cb * P : (cb + 1) * P], rhs=e[b][:, chunk(jc)],
+                            start=(b == 0), stop=(b == UB - 1),
+                        )
+                    v = chunks.tile([P, BANK], F32, name="v")
+                    nc.vector.tensor_tensor(v[:], v_ps[:], inv_sum[jc][:], ALU.mult)
+                    nc.scalar.activation(out=p[:, chunk(jc)], in_=v[:], func=ACT.Relu)
+                    exp_v = chunks.tile([P, BANK], F32, name="exp_v")
+                    nc.scalar.activation(out=exp_v[:], in_=v[:], func=ACT.Exp)
+                    nc.vector.tensor_scalar(
+                        out=q[:, chunk(jc)], in0=exp_v[:], scalar1=1.0, scalar2=-1.0,
+                        op0=ALU.min, op1=ALU.add,
+                    )
+                window = next_windows[cb]
+                nc.vector.tensor_tensor(window[:].indirect(offsets[:]), p[:], q[:], ALU.add)
+                nc.sync.dma_start(out[cb * P : (cb + 1) * P, :], window[:])
+                if cb + 2 < CB:
+                    next_windows.append(load_window(cb + 2))

@@ -25,7 +25,6 @@ def tile_sparsegraphattention_b_kernel(tc, x, w, attn_src, attn_dst, adj_t, base
     nc = tc.nc
     with (
         tc.tile_pool(name="held", bufs=1) as held,
-        tc.tile_pool(name="windows", bufs=2) as windows,
         tc.psum_pool(name="banks", bufs=8) as banks,
     ):
         def bank(name):
@@ -34,22 +33,18 @@ def tile_sparsegraphattention_b_kernel(tc, x, w, attn_src, attn_dst, adj_t, base
         def chunk(jc):
             return slice(jc * BANK, (jc + 1) * BANK)
 
-        def load_window(cb):
-            window = windows.tile([P, SLOTS], F32, name="window")
-            nc.sync.dma_start(window[:], base[cb * P : (cb + 1) * P, :])
-            return window
+        def half(side):
+            return slice(side * (N // 2), (side + 1) * (N // 2))
 
         offsets = held.tile([P, N // 16], U16, name="offsets")
-        nc.sync.dma_start(offsets[:], offs)
-
         h_t = [held.tile([P, C], BF16, name=f"h_t{b}") for b in range(UB)]
         e = [held.tile([P, N], BF16, name=f"e{b}") for b in range(UB)]
-        inv_sum = [held.tile([P, BANK], F32, name=f"inv_sum{jc}") for jc in range(JC)]
+        inv_sum = held.tile([P, N], F32, name="inv_sum")
 
         with (
             tc.tile_pool(name="early", bufs=1) as early,
             tc.tile_pool(name="scratch", bufs=2) as scratch,
-            tc.tile_pool(name="adjacency", bufs=5) as adjacency,
+            tc.tile_pool(name="adjacency", bufs=8) as adjacency,
             tc.tile_pool(name="second_terms", bufs=3) as second_terms,
         ):
             w_sb = early.tile([P, KB, C], BF16, name="w_sb")
@@ -57,13 +52,15 @@ def tile_sparsegraphattention_b_kernel(tc, x, w, attn_src, attn_dst, adj_t, base
             attn_rows = []
             for name, vector in (("dst", attn_dst), ("src", attn_src)):
                 row = early.tile([P, C], BF16, name=f"attn_{name}_row")
-                nc.sync.dma_start(row[:], vector.rearrange("c one -> (c one)").partition_broadcast(P))
+                nc.scalar.dma_start(row[:], vector.rearrange("c one -> (c one)").partition_broadcast(P))
                 attn_rows.append(row)
             x_panels = []
             for jc in range(JC):
                 panel = early.tile([P, KB, BANK], BF16, name=f"x_panel{jc}")
-                nc.sync.dma_start(panel[:], x[:, chunk(jc)].rearrange("(kb p) u -> p kb u", p=P))
+                queue = nc.sync if jc % 2 == 0 else nc.scalar
+                queue.dma_start(panel[:], x[:, chunk(jc)].rearrange("(kb p) u -> p kb u", p=P))
                 x_panels.append(panel)
+            nc.sync.dma_start(offsets[:], offs)
 
             def x_block(b, kb):
                 first = (b % UB_PER_PANEL) * P
@@ -74,18 +71,22 @@ def tile_sparsegraphattention_b_kernel(tc, x, w, attn_src, attn_dst, adj_t, base
             identity = early.tile([P, P], F32, name="identity")
             make_identity(nc, identity[:])
 
-            w_attn = early.tile([P, 2, KB], F32, name="w_attn")
-            for v, row in enumerate(attn_rows):
+            def w_times(row, name):
+                sums = early.tile([P, KB], F32, name=name)
                 for kb in range(KB):
                     products = scratch.tile([P, C], F32, name="products")
                     nc.vector.scalar_tensor_tensor(
                         out=products[:], in0=w_sb[:, kb, :], scalar=1.0, in1=row[:],
-                        op0=ALU.mult, op1=ALU.mult, accum_out=w_attn[:, v, kb : kb + 1],
+                        op0=ALU.mult, op1=ALU.mult, accum_out=sums[:, kb : kb + 1],
                     )
+                return sums
+
+            w_attn_dst = w_times(attn_rows[0], "w_attn_dst")
             w_dst_cols = early.tile([P, KB, P], BF16, name="w_dst_cols")
-            nc.vector.tensor_copy(w_dst_cols[:], w_attn[:, 0, :].unsqueeze(2).to_broadcast([P, KB, P]))
+            nc.vector.tensor_copy(w_dst_cols[:], w_attn_dst[:].unsqueeze(2).to_broadcast([P, KB, P]))
+            w_attn_src = w_times(attn_rows[1], "w_attn_src")
             w_src_col = early.tile([P, KB], BF16, name="w_src_col")
-            nc.vector.tensor_copy(w_src_col[:], w_attn[:, 1, :])
+            nc.vector.tensor_copy(w_src_col[:], w_attn_src[:])
 
             a_dst_rows = early.tile([P, N], F32, name="a_dst_rows")
             for jc in range(JC):
@@ -135,7 +136,7 @@ def tile_sparsegraphattention_b_kernel(tc, x, w, attn_src, attn_dst, adj_t, base
                         h_ps[:], lhsT=x_block(b, kb), rhs=w_sb[:, kb, :],
                         start=(kb == 0), stop=(kb == KB - 1),
                     )
-                nc.scalar.copy(h_t[b][:], h_ps[:])
+                nc.vector.tensor_copy(h_t[b][:], h_ps[:])
 
             sum_ps = [bank(f"sum_ps{jc}") for jc in range(JC)]
             for b in range(UB):
@@ -155,18 +156,25 @@ def tile_sparsegraphattention_b_kernel(tc, x, w, attn_src, attn_dst, adj_t, base
                         sum_ps[jc][:], lhsT=ones[:], rhs=e[b][:, chunk(jc)],
                         start=(b == 0), stop=(b == UB - 1),
                     )
-            next_windows = [load_window(0), load_window(1)]
 
+            ln_sum = held.tile([P, N], F32, name="ln_sum")
             for jc in range(JC):
-                nc.scalar.activation(out=inv_sum[jc][:], in_=sum_ps[jc][:], func=ACT.Ln)
-            for jc in range(JC):
-                nc.scalar.activation(out=inv_sum[jc][:], in_=inv_sum[jc][:], func=ACT.Exp, scale=-1.0)
+                nc.scalar.activation(out=ln_sum[:, chunk(jc)], in_=sum_ps[jc][:], func=ACT.Ln)
+            nc.scalar.activation(out=inv_sum[:], in_=ln_sum[:], func=ACT.Exp, scale=-1.0)
 
         with (
+            tc.tile_pool(name="windows", bufs=2) as windows,
             tc.tile_pool(name="addends", bufs=2) as addends,
-            tc.tile_pool(name="chunks", bufs=3) as chunks,
         ):
+            def load_window(cb):
+                window = windows.tile([P, SLOTS], F32, name="window")
+                nc.sync.dma_start(window[:], base[cb * P : (cb + 1) * P, :])
+                return window
+
+            next_windows = [load_window(0), load_window(1)]
             for cb in range(CB):
+                v = addends.tile([P, N], F32, name="v")
+                exp_v = addends.tile([P, N], F32, name="exp_v")
                 p = addends.tile([P, N], F32, name="p")
                 q = addends.tile([P, N], F32, name="q")
                 for jc in range(JC):
@@ -176,13 +184,13 @@ def tile_sparsegraphattention_b_kernel(tc, x, w, attn_src, attn_dst, adj_t, base
                             v_ps[:], lhsT=h_t[b][:, cb * P : (cb + 1) * P], rhs=e[b][:, chunk(jc)],
                             start=(b == 0), stop=(b == UB - 1),
                         )
-                    v = chunks.tile([P, BANK], F32, name="v")
-                    nc.vector.tensor_tensor(v[:], v_ps[:], inv_sum[jc][:], ALU.mult)
-                    nc.scalar.activation(out=p[:, chunk(jc)], in_=v[:], func=ACT.Relu)
-                    exp_v = chunks.tile([P, BANK], F32, name="exp_v")
-                    nc.scalar.activation(out=exp_v[:], in_=v[:], func=ACT.Exp)
+                    nc.vector.tensor_tensor(v[:, chunk(jc)], v_ps[:], inv_sum[:, chunk(jc)], ALU.mult)
+                    if jc % 2 == 1:
+                        nc.scalar.activation(out=exp_v[:, half(jc // 2)], in_=v[:, half(jc // 2)], func=ACT.Exp)
+                nc.vector.tensor_scalar_max(p[:], v[:], 0.0)
+                for side in range(2):
                     nc.vector.tensor_scalar(
-                        out=q[:, chunk(jc)], in0=exp_v[:], scalar1=1.0, scalar2=-1.0,
+                        out=q[:, half(side)], in0=exp_v[:, half(side)], scalar1=1.0, scalar2=-1.0,
                         op0=ALU.min, op1=ALU.add,
                     )
                 window = next_windows[cb]

@@ -1,5 +1,4 @@
 import concourse.mybir as mybir
-from concourse.masks import make_identity
 
 F32 = mybir.dt.float32
 BF16 = mybir.dt.bfloat16
@@ -17,6 +16,7 @@ CB = C // P
 UB = N // P
 JC = N // BANK
 UB_PER_PANEL = BANK // P
+BLOCKS_AHEAD = 2
 
 FLOPS = 2 * F * C * N + 2 * 2 * C * N + 2 * C * N * N
 
@@ -45,7 +45,6 @@ def tile_sparsegraphattention_b_kernel(tc, x, w, attn_src, attn_dst, adj_t, base
             tc.tile_pool(name="early", bufs=1) as early,
             tc.tile_pool(name="scratch", bufs=2) as scratch,
             tc.tile_pool(name="adjacency", bufs=8) as adjacency,
-            tc.tile_pool(name="second_terms", bufs=3) as second_terms,
         ):
             w_sb = early.tile([P, KB, C], BF16, name="w_sb")
             nc.sync.dma_start(w_sb[:], w.rearrange("(kb p) c -> p kb c", p=P))
@@ -66,10 +65,6 @@ def tile_sparsegraphattention_b_kernel(tc, x, w, attn_src, attn_dst, adj_t, base
                 first = (b % UB_PER_PANEL) * P
                 return x_panels[b // UB_PER_PANEL][:, kb, first : first + P]
 
-            ones = early.tile([P, P], BF16, name="ones")
-            nc.vector.memset(ones[:], 1.0)
-            identity = early.tile([P, P], F32, name="identity")
-            make_identity(nc, identity[:])
 
             def w_times(row, name):
                 sums = early.tile([P, KB], F32, name=name)
@@ -88,7 +83,18 @@ def tile_sparsegraphattention_b_kernel(tc, x, w, attn_src, attn_dst, adj_t, base
             w_src_col = early.tile([P, KB], BF16, name="w_src_col")
             nc.vector.tensor_copy(w_src_col[:], w_attn_src[:])
 
+            def project(b):
+                h_ps = bank(f"h_ps{b}")
+                for kb in range(KB):
+                    nc.tensor.matmul(
+                        h_ps[:], lhsT=x_block(b, kb), rhs=w_sb[:, kb, :], start=(kb == 0), stop=(kb == KB - 1)
+                    )
+                return h_ps
+
+            h_banks = [project(b) for b in range(BLOCKS_AHEAD)]
+
             a_dst_rows = early.tile([P, N], F32, name="a_dst_rows")
+            chunk_low = early.tile([P, JC], F32, name="chunk_low")
             for jc in range(JC):
                 a_dst_ps = bank(f"a_dst_ps{jc}")
                 for kb in range(KB):
@@ -97,6 +103,16 @@ def tile_sparsegraphattention_b_kernel(tc, x, w, attn_src, attn_dst, adj_t, base
                         start=(kb == 0), stop=(kb == KB - 1),
                     )
                 nc.scalar.copy(a_dst_rows[:, chunk(jc)], a_dst_ps[:])
+                nc.vector.tensor_reduce(out=chunk_low[:, jc : jc + 1], in_=a_dst_ps[:], axis=AXIS_X, op=ALU.min)
+            low = early.tile([P, 1], F32, name="low")
+            nc.vector.tensor_reduce(out=low[:], in_=chunk_low[:], axis=AXIS_X, op=ALU.min)
+
+            receiver_bias = early.tile([P, 1], F32, name="receiver_bias")
+            nc.vector.tensor_scalar_mul(receiver_bias[:], low[:], 1.0 - SLOPE)
+            receiver_rows = early.tile([P, N], F32, name="receiver_rows")
+            nc.scalar.activation(
+                out=receiver_rows[:], in_=a_dst_rows[:], func=ACT.Exp, bias=receiver_bias[:, 0:1], scale=SLOPE - 1.0
+            )
 
             a_src_ps = bank("a_src_ps")
             for b in range(UB):
@@ -105,62 +121,39 @@ def tile_sparsegraphattention_b_kernel(tc, x, w, attn_src, attn_dst, adj_t, base
                         a_src_ps[:, b : b + 1], lhsT=x_block(b, kb), rhs=w_src_col[:, kb : kb + 1],
                         start=(kb == 0), stop=(kb == KB - 1),
                     )
-            a_src = early.tile([P, UB], F32, name="a_src")
-            nc.vector.tensor_copy(a_src[:], a_src_ps[:, 0:UB])
-
-            own_max = early.tile([P, 1], F32, name="own_max")
-            nc.vector.reduce_max(out=own_max[:], in_=a_src[:], axis=AXIS_X)
-            own_max_cols = early.tile([P, P], F32, name="own_max_cols")
-            nc.vector.tensor_copy(own_max_cols[:], own_max[:].to_broadcast([P, P]))
-            maxima_ps = bank("maxima_ps")
-            nc.tensor.matmul(maxima_ps[:, 0:P], lhsT=own_max_cols[:], rhs=identity[:], start=True, stop=True)
-            top = early.tile([P, 1], F32, name="top")
-            nc.vector.reduce_max(out=top[:], in_=maxima_ps[:, 0:P], axis=AXIS_X)
-
-            shifted = early.tile([P, UB], F32, name="shifted")
-            nc.vector.tensor_scalar(
-                out=shifted[:], in0=a_src[:], scalar1=top[:, 0:1], scalar2=None, op0=ALU.subtract
-            )
-            first_term = early.tile([P, UB], F32, name="first_term")
-            nc.scalar.activation(out=first_term[:], in_=shifted[:], func=ACT.Exp)
-            second_bias = early.tile([P, UB], F32, name="second_bias")
-            nc.vector.tensor_scalar(
-                out=second_bias[:], in0=a_src[:], scalar1=SLOPE, scalar2=top[:, 0:1],
-                op0=ALU.mult, op1=ALU.subtract,
-            )
+            d = early.tile([P, UB], F32, name="d")
+            nc.vector.tensor_scalar_add(d[:], a_src_ps[:, 0:UB], low[:, 0:1])
+            sender_floor = early.tile([P, UB], F32, name="sender_floor")
+            nc.scalar.activation(out=sender_floor[:], in_=d[:], func=ACT.Exp, scale=1.0 - SLOPE)
+            sender_factor = early.tile([P, UB], F32, name="sender_factor")
+            nc.scalar.activation(out=sender_factor[:], in_=d[:], func=ACT.Exp, scale=SLOPE)
+            factor_cols = early.tile([P, UB, P], BF16, name="factor_cols")
+            nc.vector.tensor_copy(factor_cols[:], sender_factor[:].unsqueeze(2).to_broadcast([P, UB, P]))
 
             for b in range(UB):
-                h_ps = bank(f"h_ps{b}")
-                for kb in range(KB):
-                    nc.tensor.matmul(
-                        h_ps[:], lhsT=x_block(b, kb), rhs=w_sb[:, kb, :],
-                        start=(kb == 0), stop=(kb == KB - 1),
-                    )
-                nc.vector.tensor_copy(h_t[b][:], h_ps[:])
+                if b >= BLOCKS_AHEAD:
+                    h_banks.append(project(b))
+                nc.scalar.activation(out=h_t[b][:], in_=h_banks[b][:], func=ACT.Copy, scale=sender_factor[:, b : b + 1])
 
             sum_ps = [bank(f"sum_ps{jc}") for jc in range(JC)]
             for b in range(UB):
                 adj = adjacency.tile([P, N], F32, name="adj")
                 nc.sync.dma_start(adj[:], adj_t[b * P : (b + 1) * P, :])
-                second_term = second_terms.tile([P, N], F32, name="second_term")
-                nc.scalar.activation(
-                    out=second_term[:], in_=a_dst_rows[:], func=ACT.Exp,
-                    bias=second_bias[:, b : b + 1], scale=SLOPE - 1.0,
-                )
                 nc.vector.scalar_tensor_tensor(
-                    out=e[b][:], in0=second_term[:], scalar=first_term[:, b : b + 1], in1=adj[:],
+                    out=e[b][:], in0=receiver_rows[:], scalar=sender_floor[:, b : b + 1], in1=adj[:],
                     op0=ALU.max, op1=ALU.mult,
                 )
                 for jc in range(JC):
                     nc.tensor.matmul(
-                        sum_ps[jc][:], lhsT=ones[:], rhs=e[b][:, chunk(jc)],
+                        sum_ps[jc][:], lhsT=factor_cols[:, b, :], rhs=e[b][:, chunk(jc)],
                         start=(b == 0), stop=(b == UB - 1),
                     )
 
             ln_sum = held.tile([P, N], F32, name="ln_sum")
             for jc in range(JC):
                 nc.scalar.activation(out=ln_sum[:, chunk(jc)], in_=sum_ps[jc][:], func=ACT.Ln)
-            nc.scalar.activation(out=inv_sum[:], in_=ln_sum[:], func=ACT.Exp, scale=-1.0)
+            for side in range(2):
+                nc.scalar.activation(out=inv_sum[:, half(side)], in_=ln_sum[:, half(side)], func=ACT.Exp, scale=-1.0)
 
         with (
             tc.tile_pool(name="windows", bufs=2) as windows,

@@ -11,6 +11,7 @@ P = 128
 F, C, N, SLOTS = 512, 512, 2048, 4096
 SLOPE = 0.2
 BANK = 512
+PSUM_BANKS = 8
 KB = F // P
 CB = C // P
 UB = N // P
@@ -25,7 +26,7 @@ def tile_sparsegraphattention_b_kernel(tc, x, w, attn_src, attn_dst, adj_t, base
     nc = tc.nc
     with (
         tc.tile_pool(name="held", bufs=1) as held,
-        tc.psum_pool(name="banks", bufs=8) as banks,
+        tc.psum_pool(name="banks", bufs=PSUM_BANKS) as banks,
     ):
         def bank(name):
             return banks.tile([P, BANK], F32, tag="bank", name=name)
@@ -36,9 +37,13 @@ def tile_sparsegraphattention_b_kernel(tc, x, w, attn_src, attn_dst, adj_t, base
         def half(side):
             return slice(side * (N // 2), (side + 1) * (N // 2))
 
+        def repeated(column):
+            return column.to_broadcast([P, P])
+
         offsets = held.tile([P, N // 16], U16, name="offsets")
         h_t = [held.tile([P, C], BF16, name=f"h_t{b}") for b in range(UB)]
-        e = [held.tile([P, N], BF16, name=f"e{b}") for b in range(UB)]
+        t = [held.tile([P, N], BF16, name=f"t{b}") for b in range(UB)]
+        ln_sum = held.tile([P, N], F32, name="ln_sum")
         inv_sum = held.tile([P, N], F32, name="inv_sum")
 
         with (
@@ -48,11 +53,14 @@ def tile_sparsegraphattention_b_kernel(tc, x, w, attn_src, attn_dst, adj_t, base
         ):
             w_sb = early.tile([P, KB, C], BF16, name="w_sb")
             nc.sync.dma_start(w_sb[:], w.rearrange("(kb p) c -> p kb c", p=P))
-            attn_rows = []
-            for name, vector in (("dst", attn_dst), ("src", attn_src)):
-                row = early.tile([P, C], BF16, name=f"attn_{name}_row")
-                nc.scalar.dma_start(row[:], vector.rearrange("c one -> (c one)").partition_broadcast(P))
-                attn_rows.append(row)
+
+            def as_rows(vector, name):
+                rows = early.tile([P, C], BF16, name=name)
+                nc.scalar.dma_start(rows[:], vector.rearrange("c one -> (c one)").partition_broadcast(P))
+                return rows
+
+            attn_dst_rows = as_rows(attn_dst, "attn_dst_rows")
+            attn_src_rows = as_rows(attn_src, "attn_src_rows")
             x_panels = []
             for jc in range(JC):
                 panel = early.tile([P, KB, BANK], BF16, name=f"x_panel{jc}")
@@ -65,23 +73,20 @@ def tile_sparsegraphattention_b_kernel(tc, x, w, attn_src, attn_dst, adj_t, base
                 first = (b % UB_PER_PANEL) * P
                 return x_panels[b // UB_PER_PANEL][:, kb, first : first + P]
 
-
-            def w_times(row, name):
-                sums = early.tile([P, KB], F32, name=name)
+            def w_times(rows, name):
+                sums = early.tile([P, KB], F32, name=f"{name}_f32")
                 for kb in range(KB):
                     products = scratch.tile([P, C], F32, name="products")
                     nc.vector.scalar_tensor_tensor(
-                        out=products[:], in0=w_sb[:, kb, :], scalar=1.0, in1=row[:],
+                        out=products[:], in0=w_sb[:, kb, :], scalar=1.0, in1=rows[:],
                         op0=ALU.mult, op1=ALU.mult, accum_out=sums[:, kb : kb + 1],
                     )
-                return sums
+                rounded = early.tile([P, KB], BF16, name=name)
+                nc.vector.tensor_copy(rounded[:], sums[:])
+                return rounded
 
-            w_attn_dst = w_times(attn_rows[0], "w_attn_dst")
-            w_dst_cols = early.tile([P, KB, P], BF16, name="w_dst_cols")
-            nc.vector.tensor_copy(w_dst_cols[:], w_attn_dst[:].unsqueeze(2).to_broadcast([P, KB, P]))
-            w_attn_src = w_times(attn_rows[1], "w_attn_src")
-            w_src_col = early.tile([P, KB], BF16, name="w_src_col")
-            nc.vector.tensor_copy(w_src_col[:], w_attn_src[:])
+            w_attn_dst = w_times(attn_dst_rows, "w_attn_dst")
+            w_attn_src = w_times(attn_src_rows, "w_attn_src")
 
             def project(b):
                 h_ps = bank(f"h_ps{b}")
@@ -99,7 +104,7 @@ def tile_sparsegraphattention_b_kernel(tc, x, w, attn_src, attn_dst, adj_t, base
                 a_dst_ps = bank(f"a_dst_ps{jc}")
                 for kb in range(KB):
                     nc.tensor.matmul(
-                        a_dst_ps[:], lhsT=w_dst_cols[:, kb, :], rhs=x_panels[jc][:, kb, :],
+                        a_dst_ps[:], lhsT=repeated(w_attn_dst[:, kb : kb + 1]), rhs=x_panels[jc][:, kb, :],
                         start=(kb == 0), stop=(kb == KB - 1),
                     )
                 nc.scalar.copy(a_dst_rows[:, chunk(jc)], a_dst_ps[:])
@@ -118,38 +123,37 @@ def tile_sparsegraphattention_b_kernel(tc, x, w, attn_src, attn_dst, adj_t, base
             for b in range(UB):
                 for kb in range(KB):
                     nc.tensor.matmul(
-                        a_src_ps[:, b : b + 1], lhsT=x_block(b, kb), rhs=w_src_col[:, kb : kb + 1],
+                        a_src_ps[:, b : b + 1], lhsT=x_block(b, kb), rhs=w_attn_src[:, kb : kb + 1],
                         start=(kb == 0), stop=(kb == KB - 1),
                     )
             d = early.tile([P, UB], F32, name="d")
             nc.vector.tensor_scalar_add(d[:], a_src_ps[:, 0:UB], low[:, 0:1])
             sender_floor = early.tile([P, UB], F32, name="sender_floor")
             nc.scalar.activation(out=sender_floor[:], in_=d[:], func=ACT.Exp, scale=1.0 - SLOPE)
-            sender_factor = early.tile([P, UB], F32, name="sender_factor")
-            nc.scalar.activation(out=sender_factor[:], in_=d[:], func=ACT.Exp, scale=SLOPE)
-            factor_cols = early.tile([P, UB, P], BF16, name="factor_cols")
-            nc.vector.tensor_copy(factor_cols[:], sender_factor[:].unsqueeze(2).to_broadcast([P, UB, P]))
+            factor = early.tile([P, UB], F32, name="factor")
+            nc.scalar.activation(out=factor[:], in_=d[:], func=ACT.Exp, scale=SLOPE)
+            factor_bf16 = early.tile([P, UB], BF16, name="factor_bf16")
+            nc.scalar.activation(out=factor_bf16[:], in_=d[:], func=ACT.Exp, scale=SLOPE)
 
             for b in range(UB):
                 if b >= BLOCKS_AHEAD:
                     h_banks.append(project(b))
-                nc.scalar.activation(out=h_t[b][:], in_=h_banks[b][:], func=ACT.Copy, scale=sender_factor[:, b : b + 1])
+                nc.scalar.activation(out=h_t[b][:], in_=h_banks[b][:], func=ACT.Copy, scale=factor[:, b : b + 1])
 
             sum_ps = [bank(f"sum_ps{jc}") for jc in range(JC)]
             for b in range(UB):
                 adj = adjacency.tile([P, N], F32, name="adj")
                 nc.sync.dma_start(adj[:], adj_t[b * P : (b + 1) * P, :])
                 nc.vector.scalar_tensor_tensor(
-                    out=e[b][:], in0=receiver_rows[:], scalar=sender_floor[:, b : b + 1], in1=adj[:],
+                    out=t[b][:], in0=receiver_rows[:], scalar=sender_floor[:, b : b + 1], in1=adj[:],
                     op0=ALU.max, op1=ALU.mult,
                 )
                 for jc in range(JC):
                     nc.tensor.matmul(
-                        sum_ps[jc][:], lhsT=factor_cols[:, b, :], rhs=e[b][:, chunk(jc)],
+                        sum_ps[jc][:], lhsT=repeated(factor_bf16[:, b : b + 1]), rhs=t[b][:, chunk(jc)],
                         start=(b == 0), stop=(b == UB - 1),
                     )
 
-            ln_sum = held.tile([P, N], F32, name="ln_sum")
             for jc in range(JC):
                 nc.scalar.activation(out=ln_sum[:, chunk(jc)], in_=sum_ps[jc][:], func=ACT.Ln)
             for side in range(2):
@@ -164,7 +168,7 @@ def tile_sparsegraphattention_b_kernel(tc, x, w, attn_src, attn_dst, adj_t, base
                 nc.sync.dma_start(window[:], base[cb * P : (cb + 1) * P, :])
                 return window
 
-            next_windows = [load_window(0), load_window(1)]
+            loaded = [load_window(0), load_window(1)]
             for cb in range(CB):
                 v = addends.tile([P, N], F32, name="v")
                 exp_v = addends.tile([P, N], F32, name="exp_v")
@@ -174,7 +178,7 @@ def tile_sparsegraphattention_b_kernel(tc, x, w, attn_src, attn_dst, adj_t, base
                     v_ps = bank(f"v_ps{cb}_{jc}")
                     for b in range(UB):
                         nc.tensor.matmul(
-                            v_ps[:], lhsT=h_t[b][:, cb * P : (cb + 1) * P], rhs=e[b][:, chunk(jc)],
+                            v_ps[:], lhsT=h_t[b][:, cb * P : (cb + 1) * P], rhs=t[b][:, chunk(jc)],
                             start=(b == 0), stop=(b == UB - 1),
                         )
                     nc.vector.tensor_tensor(v[:, chunk(jc)], v_ps[:], inv_sum[:, chunk(jc)], ALU.mult)
@@ -186,8 +190,7 @@ def tile_sparsegraphattention_b_kernel(tc, x, w, attn_src, attn_dst, adj_t, base
                         out=q[:, half(side)], in0=exp_v[:, half(side)], scalar1=1.0, scalar2=-1.0,
                         op0=ALU.min, op1=ALU.add,
                     )
-                window = next_windows[cb]
-                nc.vector.tensor_tensor(window[:].indirect(offsets[:]), p[:], q[:], ALU.add)
-                nc.sync.dma_start(out[cb * P : (cb + 1) * P, :], window[:])
+                nc.vector.tensor_tensor(loaded[cb][:].indirect(offsets[:]), p[:], q[:], ALU.add)
+                nc.sync.dma_start(out[cb * P : (cb + 1) * P, :], loaded[cb][:])
                 if cb + 2 < CB:
-                    next_windows.append(load_window(cb + 2))
+                    loaded.append(load_window(cb + 2))

@@ -1,4 +1,5 @@
 import concourse.mybir as mybir
+from concourse.masks import make_identity
 
 F32 = mybir.dt.float32
 BF16 = mybir.dt.bfloat16
@@ -11,10 +12,13 @@ P = 128
 F, C, N, SLOTS = 512, 512, 2048, 4096
 SLOPE = 0.2
 BANK = 512
-PSUM_BANKS = 8
+WIDE_BANKS = 6
+SIDE_BANKS = 2
 KB = F // P
 CB = C // P
 UB = N // P
+JB = N // P
+JB_PER_BANK = BANK // P
 JC = N // BANK
 UB_PER_PANEL = BANK // P
 BLOCKS_AHEAD = 2
@@ -26,10 +30,15 @@ def tile_sparsegraphattention_b_kernel(tc, x, w, attn_src, attn_dst, adj_t, base
     nc = tc.nc
     with (
         tc.tile_pool(name="held", bufs=1) as held,
-        tc.psum_pool(name="banks", bufs=PSUM_BANKS) as banks,
+        tc.tile_pool(name="windows", bufs=2) as windows,
+        tc.psum_pool(name="banks", bufs=WIDE_BANKS) as banks,
+        tc.psum_pool(name="side_banks", bufs=SIDE_BANKS) as side_banks,
     ):
         def bank(name):
             return banks.tile([P, BANK], F32, tag="bank", name=name)
+
+        def side_bank(name):
+            return side_banks.tile([P, BANK], F32, tag="side_bank", name=name)
 
         def chunk(jc):
             return slice(jc * BANK, (jc + 1) * BANK)
@@ -40,11 +49,19 @@ def tile_sparsegraphattention_b_kernel(tc, x, w, attn_src, attn_dst, adj_t, base
         def repeated(column):
             return column.to_broadcast([P, P])
 
+        def load_window(cb):
+            window = windows.tile([P, SLOTS], F32, name="window")
+            nc.sync.dma_start(window[:], base[cb * P : (cb + 1) * P, :])
+            return window
+
         offsets = held.tile([P, N // 16], U16, name="offsets")
         h_t = [held.tile([P, C], BF16, name=f"h_t{b}") for b in range(UB)]
         t = [held.tile([P, N], BF16, name=f"t{b}") for b in range(UB)]
-        ln_sum = held.tile([P, N], F32, name="ln_sum")
+        sum_cols = held.tile([P, JB], F32, name="sum_cols")
+        inv_cols = held.tile([P, JB], F32, name="inv_cols")
         inv_sum = held.tile([P, N], F32, name="inv_sum")
+        identity = held.tile([P, P], F32, name="identity")
+        make_identity(nc, identity[:])
 
         with (
             tc.tile_pool(name="early", bufs=1) as early,
@@ -101,7 +118,7 @@ def tile_sparsegraphattention_b_kernel(tc, x, w, attn_src, attn_dst, adj_t, base
             a_dst_rows = early.tile([P, N], F32, name="a_dst_rows")
             chunk_low = early.tile([P, JC], F32, name="chunk_low")
             for jc in range(JC):
-                a_dst_ps = bank(f"a_dst_ps{jc}")
+                a_dst_ps = side_bank(f"a_dst_ps{jc}")
                 for kb in range(KB):
                     nc.tensor.matmul(
                         a_dst_ps[:], lhsT=repeated(w_attn_dst[:, kb : kb + 1]), rhs=x_panels[jc][:, kb, :],
@@ -119,7 +136,7 @@ def tile_sparsegraphattention_b_kernel(tc, x, w, attn_src, attn_dst, adj_t, base
                 out=receiver_rows[:], in_=a_dst_rows[:], func=ACT.Exp, bias=receiver_bias[:, 0:1], scale=SLOPE - 1.0
             )
 
-            a_src_ps = bank("a_src_ps")
+            a_src_ps = side_bank("a_src_ps")
             for b in range(UB):
                 for kb in range(KB):
                     nc.tensor.matmul(
@@ -140,7 +157,7 @@ def tile_sparsegraphattention_b_kernel(tc, x, w, attn_src, attn_dst, adj_t, base
                     h_banks.append(project(b))
                 nc.scalar.activation(out=h_t[b][:], in_=h_banks[b][:], func=ACT.Copy, scale=factor[:, b : b + 1])
 
-            sum_ps = [bank(f"sum_ps{jc}") for jc in range(JC)]
+            part_sums = side_bank("part_sums")
             for b in range(UB):
                 adj = adjacency.tile([P, N], F32, name="adj")
                 nc.sync.dma_start(adj[:], adj_t[b * P : (b + 1) * P, :])
@@ -148,27 +165,29 @@ def tile_sparsegraphattention_b_kernel(tc, x, w, attn_src, attn_dst, adj_t, base
                     out=t[b][:], in0=receiver_rows[:], scalar=sender_floor[:, b : b + 1], in1=adj[:],
                     op0=ALU.max, op1=ALU.mult,
                 )
-                for jc in range(JC):
+                for jb in range(JB):
                     nc.tensor.matmul(
-                        sum_ps[jc][:], lhsT=repeated(factor_bf16[:, b : b + 1]), rhs=t[b][:, chunk(jc)],
-                        start=(b == 0), stop=(b == UB - 1),
+                        part_sums[:, jb * UB + b : jb * UB + b + 1], lhsT=t[b][:, jb * P : (jb + 1) * P],
+                        rhs=factor_bf16[:, b : b + 1], start=True, stop=True,
                     )
 
-            for jc in range(JC):
-                nc.scalar.activation(out=ln_sum[:, chunk(jc)], in_=sum_ps[jc][:], func=ACT.Ln)
-            for side in range(2):
-                nc.scalar.activation(out=inv_sum[:, half(side)], in_=ln_sum[:, half(side)], func=ACT.Exp, scale=-1.0)
-
-        with (
-            tc.tile_pool(name="windows", bufs=2) as windows,
-            tc.tile_pool(name="addends", bufs=2) as addends,
-        ):
-            def load_window(cb):
-                window = windows.tile([P, SLOTS], F32, name="window")
-                nc.sync.dma_start(window[:], base[cb * P : (cb + 1) * P, :])
-                return window
-
             loaded = [load_window(0), load_window(1)]
+
+            nc.vector.tensor_reduce(
+                out=sum_cols[:], in_=part_sums[:, 0 : JB * UB].rearrange("p (jb b) -> p jb b", b=UB), axis=AXIS_X, op=ALU.add
+            )
+            nc.vector.reciprocal(inv_cols[:], sum_cols[:])
+            for jc in range(JC):
+                inv_ps = side_bank(f"inv_ps{jc}")
+                for k in range(JB_PER_BANK):
+                    jb = jc * JB_PER_BANK + k
+                    nc.tensor.matmul(
+                        inv_ps[:, k * P : (k + 1) * P], lhsT=repeated(inv_cols[:, jb : jb + 1]), rhs=identity[:],
+                        start=True, stop=True,
+                    )
+                nc.scalar.copy(inv_sum[:, chunk(jc)], inv_ps[:])
+
+        with tc.tile_pool(name="addends", bufs=2) as addends:
             for cb in range(CB):
                 v = addends.tile([P, N], F32, name="v")
                 exp_v = addends.tile([P, N], F32, name="exp_v")

@@ -19,9 +19,10 @@ CB = C // P
 UB = N // P
 JB = N // P
 JB_PER_BANK = BANK // P
+BF16_PARTS = 3
 JC = N // BANK
 UB_PER_PANEL = BANK // P
-BLOCKS_AHEAD = 2
+SRC, DST = 0, 1
 
 FLOPS = 2 * F * C * N + 2 * 2 * C * N + 2 * C * N * N
 
@@ -49,6 +50,17 @@ def tile_sparsegraphattention_b_kernel(tc, x, w, attn_src, attn_dst, adj_t, base
         def repeated(column):
             return column.to_broadcast([P, P])
 
+        def spread(parts, jc, name):
+            row_ps = side_bank(name)
+            for k in range(JB_PER_BANK):
+                jb = jc * JB_PER_BANK + k
+                for i, part in enumerate(parts):
+                    nc.tensor.matmul(
+                        row_ps[:, k * P : (k + 1) * P], lhsT=repeated(part[:, jb : jb + 1]), rhs=identity[:],
+                        start=(i == 0), stop=(i == len(parts) - 1),
+                    )
+            return row_ps
+
         def load_window(cb):
             window = windows.tile([P, SLOTS], F32, name="window")
             nc.sync.dma_start(window[:], base[cb * P : (cb + 1) * P, :])
@@ -59,8 +71,10 @@ def tile_sparsegraphattention_b_kernel(tc, x, w, attn_src, attn_dst, adj_t, base
         t = [held.tile([P, N], BF16, name=f"t{b}") for b in range(UB)]
         sum_cols = held.tile([P, JB], F32, name="sum_cols")
         inv_cols = held.tile([P, JB], F32, name="inv_cols")
+        inv_parts = [held.tile([P, JB], BF16, name=f"inv_part{i}") for i in range(BF16_PARTS)]
+        inv_rests = [held.tile([P, JB], F32, name=f"inv_rest{i}") for i in range(BF16_PARTS - 1)]
         inv_sum = held.tile([P, N], F32, name="inv_sum")
-        identity = held.tile([P, P], F32, name="identity")
+        identity = held.tile([P, P], BF16, name="identity")
         make_identity(nc, identity[:])
 
         with (
@@ -90,72 +104,65 @@ def tile_sparsegraphattention_b_kernel(tc, x, w, attn_src, attn_dst, adj_t, base
                 first = (b % UB_PER_PANEL) * P
                 return x_panels[b // UB_PER_PANEL][:, kb, first : first + P]
 
-            def w_times(rows, name):
-                sums = early.tile([P, KB], F32, name=f"{name}_f32")
-                for kb in range(KB):
+            w_attn_f32 = early.tile([P, KB, 2], F32, name="w_attn_f32")
+            for kb in range(KB):
+                for place, rows in ((SRC, attn_src_rows), (DST, attn_dst_rows)):
                     products = scratch.tile([P, C], F32, name="products")
                     nc.vector.scalar_tensor_tensor(
                         out=products[:], in0=w_sb[:, kb, :], scalar=1.0, in1=rows[:],
-                        op0=ALU.mult, op1=ALU.mult, accum_out=sums[:, kb : kb + 1],
+                        op0=ALU.mult, op1=ALU.mult, accum_out=w_attn_f32[:, kb, place : place + 1],
                     )
-                rounded = early.tile([P, KB], BF16, name=name)
-                nc.vector.tensor_copy(rounded[:], sums[:])
-                return rounded
+            w_attn = early.tile([P, KB, 2], BF16, name="w_attn")
+            nc.vector.tensor_copy(w_attn[:], w_attn_f32[:])
 
-            w_attn_dst = w_times(attn_dst_rows, "w_attn_dst")
-            w_attn_src = w_times(attn_src_rows, "w_attn_src")
+            scores_ps = side_bank("scores_ps")
+            for b in range(UB):
+                for kb in range(KB):
+                    nc.tensor.matmul(
+                        scores_ps[:, 2 * b : 2 * b + 2], lhsT=x_block(b, kb), rhs=w_attn[:, kb, :],
+                        start=(kb == 0), stop=(kb == KB - 1),
+                    )
+            for kb in range(KB):
+                nc.tensor.matmul(
+                    scores_ps[:, 2 * UB : 2 * UB + 1], lhsT=repeated(w_attn[:, kb, DST : DST + 1]),
+                    rhs=x_panels[0][:, kb, 0:1], start=(kb == 0), stop=(kb == KB - 1),
+                )
+            a_src_cols = scores_ps[:, SRC : 2 * UB : 2]
+            a_dst_cols = scores_ps[:, DST : 2 * UB : 2]
+            a_dst_0 = scores_ps[:, 2 * UB : 2 * UB + 1]
 
-            def project(b):
+            bias_steep = early.tile([P, 1], F32, name="bias_steep")
+            nc.vector.tensor_scalar_mul(bias_steep[:], a_dst_0, 1.0 - SLOPE)
+            bias_flat = early.tile([P, 1], F32, name="bias_flat")
+            nc.vector.tensor_scalar_mul(bias_flat[:], a_dst_0, SLOPE)
+            receiver_cols = early.tile([P, JB], BF16, name="receiver_cols")
+            nc.scalar.activation(
+                out=receiver_cols[:], in_=a_dst_cols, func=ACT.Exp, bias=bias_steep[:, 0:1], scale=SLOPE - 1.0
+            )
+            sender_floor = early.tile([P, UB], F32, name="sender_floor")
+            nc.scalar.activation(
+                out=sender_floor[:], in_=a_src_cols, func=ACT.Exp, bias=bias_steep[:, 0:1], scale=1.0 - SLOPE
+            )
+            factor = early.tile([P, UB], F32, name="factor")
+            nc.scalar.activation(out=factor[:], in_=a_src_cols, func=ACT.Exp, bias=bias_flat[:, 0:1], scale=SLOPE)
+            factor_bf16 = early.tile([P, UB], BF16, name="factor_bf16")
+            nc.scalar.activation(out=factor_bf16[:], in_=a_src_cols, func=ACT.Exp, bias=bias_flat[:, 0:1], scale=SLOPE)
+
+            receiver_rows = early.tile([P, N], BF16, name="receiver_rows")
+            for jc in range(JC):
+                rows_ps = spread([receiver_cols], jc, f"rows_ps{jc}")
+                if jc % 2 == 0:
+                    nc.scalar.copy(receiver_rows[:, chunk(jc)], rows_ps[:])
+                else:
+                    nc.vector.tensor_copy(receiver_rows[:, chunk(jc)], rows_ps[:])
+
+            for b in range(UB):
                 h_ps = bank(f"h_ps{b}")
                 for kb in range(KB):
                     nc.tensor.matmul(
                         h_ps[:], lhsT=x_block(b, kb), rhs=w_sb[:, kb, :], start=(kb == 0), stop=(kb == KB - 1)
                     )
-                return h_ps
-
-            h_banks = [project(b) for b in range(BLOCKS_AHEAD)]
-
-            a_dst_rows = early.tile([P, N], F32, name="a_dst_rows")
-            chunk_low = early.tile([P, JC], F32, name="chunk_low")
-            for jc in range(JC):
-                a_dst_ps = side_bank(f"a_dst_ps{jc}")
-                for kb in range(KB):
-                    nc.tensor.matmul(
-                        a_dst_ps[:], lhsT=repeated(w_attn_dst[:, kb : kb + 1]), rhs=x_panels[jc][:, kb, :],
-                        start=(kb == 0), stop=(kb == KB - 1),
-                    )
-                nc.scalar.copy(a_dst_rows[:, chunk(jc)], a_dst_ps[:])
-                nc.vector.tensor_reduce(out=chunk_low[:, jc : jc + 1], in_=a_dst_ps[:], axis=AXIS_X, op=ALU.min)
-            low = early.tile([P, 1], F32, name="low")
-            nc.vector.tensor_reduce(out=low[:], in_=chunk_low[:], axis=AXIS_X, op=ALU.min)
-
-            receiver_bias = early.tile([P, 1], F32, name="receiver_bias")
-            nc.vector.tensor_scalar_mul(receiver_bias[:], low[:], 1.0 - SLOPE)
-            receiver_rows = early.tile([P, N], F32, name="receiver_rows")
-            nc.scalar.activation(
-                out=receiver_rows[:], in_=a_dst_rows[:], func=ACT.Exp, bias=receiver_bias[:, 0:1], scale=SLOPE - 1.0
-            )
-
-            a_src_ps = side_bank("a_src_ps")
-            for b in range(UB):
-                for kb in range(KB):
-                    nc.tensor.matmul(
-                        a_src_ps[:, b : b + 1], lhsT=x_block(b, kb), rhs=w_attn_src[:, kb : kb + 1],
-                        start=(kb == 0), stop=(kb == KB - 1),
-                    )
-            d = early.tile([P, UB], F32, name="d")
-            nc.vector.tensor_scalar_add(d[:], a_src_ps[:, 0:UB], low[:, 0:1])
-            sender_floor = early.tile([P, UB], F32, name="sender_floor")
-            nc.scalar.activation(out=sender_floor[:], in_=d[:], func=ACT.Exp, scale=1.0 - SLOPE)
-            factor = early.tile([P, UB], F32, name="factor")
-            nc.scalar.activation(out=factor[:], in_=d[:], func=ACT.Exp, scale=SLOPE)
-            factor_bf16 = early.tile([P, UB], BF16, name="factor_bf16")
-            nc.scalar.activation(out=factor_bf16[:], in_=d[:], func=ACT.Exp, scale=SLOPE)
-
-            for b in range(UB):
-                if b >= BLOCKS_AHEAD:
-                    h_banks.append(project(b))
-                nc.scalar.activation(out=h_t[b][:], in_=h_banks[b][:], func=ACT.Copy, scale=factor[:, b : b + 1])
+                nc.scalar.activation(out=h_t[b][:], in_=h_ps[:], func=ACT.Copy, scale=factor[:, b : b + 1])
 
             part_sums = side_bank("part_sums")
             for b in range(UB):
@@ -177,14 +184,14 @@ def tile_sparsegraphattention_b_kernel(tc, x, w, attn_src, attn_dst, adj_t, base
                 out=sum_cols[:], in_=part_sums[:, 0 : JB * UB].rearrange("p (jb b) -> p jb b", b=UB), axis=AXIS_X, op=ALU.add
             )
             nc.vector.reciprocal(inv_cols[:], sum_cols[:])
+            rest = inv_cols
+            for i in range(BF16_PARTS):
+                nc.vector.tensor_copy(inv_parts[i][:], rest[:])
+                if i < BF16_PARTS - 1:
+                    nc.vector.tensor_tensor(inv_rests[i][:], rest[:], inv_parts[i][:], ALU.subtract)
+                    rest = inv_rests[i]
             for jc in range(JC):
-                inv_ps = side_bank(f"inv_ps{jc}")
-                for k in range(JB_PER_BANK):
-                    jb = jc * JB_PER_BANK + k
-                    nc.tensor.matmul(
-                        inv_ps[:, k * P : (k + 1) * P], lhsT=repeated(inv_cols[:, jb : jb + 1]), rhs=identity[:],
-                        start=True, stop=True,
-                    )
+                inv_ps = spread(inv_parts, jc, f"inv_ps{jc}")
                 nc.scalar.copy(inv_sum[:, chunk(jc)], inv_ps[:])
 
         with tc.tile_pool(name="addends", bufs=2) as addends:

@@ -23,6 +23,8 @@ BF16_PARTS = 3
 JC = N // BANK
 UB_PER_PANEL = BANK // P
 SRC, DST = 0, 1
+CB_PER_PART = 2
+PART = CB_PER_PART * P
 
 FLOPS = 2 * F * C * N + 2 * 2 * C * N + 2 * C * N * N
 
@@ -61,13 +63,35 @@ def tile_sparsegraphattention_b_kernel(tc, x, w, attn_src, attn_dst, adj_t, base
                     )
             return row_ps
 
+        def x_block(b, kb):
+            first = (b % UB_PER_PANEL) * P
+            return x_panels[b // UB_PER_PANEL][:, kb, first : first + P]
+
+        def project(part, free_bank):
+            for pair in range(UB // 2):
+                h_ps = free_bank(f"h_ps{part}_{pair}")
+                for i in range(2):
+                    b = 2 * pair + i
+                    for kb in range(KB):
+                        nc.tensor.matmul(
+                            h_ps[:, i * PART : (i + 1) * PART], lhsT=x_block(b, kb),
+                            rhs=w_sb[:, kb, part * PART : (part + 1) * PART], start=(kb == 0), stop=(kb == KB - 1),
+                        )
+                    nc.scalar.activation(
+                        out=h_t[part][b][:], in_=h_ps[:, i * PART : (i + 1) * PART], func=ACT.Copy,
+                        scale=factor[:, b : b + 1],
+                    )
+
         def load_window(cb):
             window = windows.tile([P, SLOTS], F32, name="window")
             nc.sync.dma_start(window[:], base[cb * P : (cb + 1) * P, :])
             return window
 
         offsets = held.tile([P, N // 16], U16, name="offsets")
-        h_t = [held.tile([P, C], BF16, name=f"h_t{b}") for b in range(UB)]
+        h_t = [[held.tile([P, PART], BF16, name=f"h_t{part}_{b}") for b in range(UB)] for part in range(C // PART)]
+        w_sb = held.tile([P, KB, C], BF16, name="w_sb")
+        x_panels = [held.tile([P, KB, BANK], BF16, name=f"x_panel{jc}") for jc in range(JC)]
+        factor = held.tile([P, UB], F32, name="factor")
         t = [held.tile([P, N], BF16, name=f"t{b}") for b in range(UB)]
         sum_cols = held.tile([P, JB], F32, name="sum_cols")
         inv_cols = held.tile([P, JB], F32, name="inv_cols")
@@ -82,7 +106,6 @@ def tile_sparsegraphattention_b_kernel(tc, x, w, attn_src, attn_dst, adj_t, base
             tc.tile_pool(name="scratch", bufs=2) as scratch,
             tc.tile_pool(name="adjacency", bufs=8) as adjacency,
         ):
-            w_sb = early.tile([P, KB, C], BF16, name="w_sb")
             nc.sync.dma_start(w_sb[:], w.rearrange("(kb p) c -> p kb c", p=P))
 
             def as_rows(vector, name):
@@ -92,21 +115,14 @@ def tile_sparsegraphattention_b_kernel(tc, x, w, attn_src, attn_dst, adj_t, base
 
             attn_dst_rows = as_rows(attn_dst, "attn_dst_rows")
             attn_src_rows = as_rows(attn_src, "attn_src_rows")
-            x_panels = []
             for jc in range(JC):
-                panel = early.tile([P, KB, BANK], BF16, name=f"x_panel{jc}")
                 queue = nc.sync if jc % 2 == 0 else nc.scalar
-                queue.dma_start(panel[:], x[:, chunk(jc)].rearrange("(kb p) u -> p kb u", p=P))
-                x_panels.append(panel)
+                queue.dma_start(x_panels[jc][:], x[:, chunk(jc)].rearrange("(kb p) u -> p kb u", p=P))
             nc.sync.dma_start(offsets[:], offs)
 
-            def x_block(b, kb):
-                first = (b % UB_PER_PANEL) * P
-                return x_panels[b // UB_PER_PANEL][:, kb, first : first + P]
-
             w_attn_f32 = early.tile([P, KB, 2], F32, name="w_attn_f32")
-            for kb in range(KB):
-                for place, rows in ((SRC, attn_src_rows), (DST, attn_dst_rows)):
+            for place, rows in ((DST, attn_dst_rows), (SRC, attn_src_rows)):
+                for kb in range(KB):
                     products = scratch.tile([P, C], F32, name="products")
                     nc.vector.scalar_tensor_tensor(
                         out=products[:], in0=w_sb[:, kb, :], scalar=1.0, in1=rows[:],
@@ -143,7 +159,6 @@ def tile_sparsegraphattention_b_kernel(tc, x, w, attn_src, attn_dst, adj_t, base
             nc.scalar.activation(
                 out=sender_floor[:], in_=a_src_cols, func=ACT.Exp, bias=bias_steep[:, 0:1], scale=1.0 - SLOPE
             )
-            factor = early.tile([P, UB], F32, name="factor")
             nc.scalar.activation(out=factor[:], in_=a_src_cols, func=ACT.Exp, bias=bias_flat[:, 0:1], scale=SLOPE)
             factor_bf16 = early.tile([P, UB], BF16, name="factor_bf16")
             nc.scalar.activation(out=factor_bf16[:], in_=a_src_cols, func=ACT.Exp, bias=bias_flat[:, 0:1], scale=SLOPE)
@@ -156,13 +171,7 @@ def tile_sparsegraphattention_b_kernel(tc, x, w, attn_src, attn_dst, adj_t, base
                 else:
                     nc.vector.tensor_copy(receiver_rows[:, chunk(jc)], rows_ps[:])
 
-            for b in range(UB):
-                h_ps = bank(f"h_ps{b}")
-                for kb in range(KB):
-                    nc.tensor.matmul(
-                        h_ps[:], lhsT=x_block(b, kb), rhs=w_sb[:, kb, :], start=(kb == 0), stop=(kb == KB - 1)
-                    )
-                nc.scalar.activation(out=h_t[b][:], in_=h_ps[:], func=ACT.Copy, scale=factor[:, b : b + 1])
+            project(0, bank)
 
             part_sums = side_bank("part_sums")
             for b in range(UB):
@@ -196,6 +205,9 @@ def tile_sparsegraphattention_b_kernel(tc, x, w, attn_src, attn_dst, adj_t, base
 
         with tc.tile_pool(name="addends", bufs=2) as addends:
             for cb in range(CB):
+                part, block = divmod(cb, CB_PER_PART)
+                if cb == CB_PER_PART - 1:
+                    project(1, side_bank)
                 v = addends.tile([P, N], F32, name="v")
                 exp_v = addends.tile([P, N], F32, name="exp_v")
                 p = addends.tile([P, N], F32, name="p")
@@ -204,7 +216,7 @@ def tile_sparsegraphattention_b_kernel(tc, x, w, attn_src, attn_dst, adj_t, base
                     v_ps = bank(f"v_ps{cb}_{jc}")
                     for b in range(UB):
                         nc.tensor.matmul(
-                            v_ps[:], lhsT=h_t[b][:, cb * P : (cb + 1) * P], rhs=t[b][:, chunk(jc)],
+                            v_ps[:], lhsT=h_t[part][b][:, block * P : (block + 1) * P], rhs=t[b][:, chunk(jc)],
                             start=(b == 0), stop=(b == UB - 1),
                         )
                     nc.vector.tensor_tensor(v[:, chunk(jc)], v_ps[:], inv_sum[:, chunk(jc)], ALU.mult)

@@ -116,8 +116,7 @@ def tile_sparsegraphattention_b_kernel(tc, x, w, attn_src, attn_dst, adj_t, base
             attn_dst_rows = as_rows(attn_dst, "attn_dst_rows")
             attn_src_rows = as_rows(attn_src, "attn_src_rows")
             for jc in range(JC):
-                queue = nc.sync if jc % 2 == 0 else nc.scalar
-                queue.dma_start(x_panels[jc][:], x[:, chunk(jc)].rearrange("(kb p) u -> p kb u", p=P))
+                nc.sync.dma_start(x_panels[jc][:], x[:, chunk(jc)].rearrange("(kb p) u -> p kb u", p=P))
             nc.sync.dma_start(offsets[:], offs)
 
             w_attn_f32 = early.tile([P, KB, 2], F32, name="w_attn_f32")

@@ -19,7 +19,6 @@ CB = C // P
 UB = N // P
 JB = N // P
 JB_PER_BANK = BANK // P
-BF16_PARTS = 3
 JC = N // BANK
 UB_PER_PANEL = BANK // P
 SRC, DST = 0, 1
@@ -52,15 +51,14 @@ def tile_sparsegraphattention_b_kernel(tc, x, w, attn_src, attn_dst, adj_t, base
         def repeated(column):
             return column.to_broadcast([P, P])
 
-        def spread(parts, jc, name):
+        def spread(cols, identity, jc, name):
             row_ps = side_bank(name)
             for k in range(JB_PER_BANK):
                 jb = jc * JB_PER_BANK + k
-                for i, part in enumerate(parts):
-                    nc.tensor.matmul(
-                        row_ps[:, k * P : (k + 1) * P], lhsT=repeated(part[:, jb : jb + 1]), rhs=identity[:],
-                        start=(i == 0), stop=(i == len(parts) - 1),
-                    )
+                nc.tensor.matmul(
+                    row_ps[:, k * P : (k + 1) * P], lhsT=repeated(cols[:, jb : jb + 1]), rhs=identity[:],
+                    start=True, stop=True,
+                )
             return row_ps
 
         def x_block(b, kb):
@@ -95,11 +93,11 @@ def tile_sparsegraphattention_b_kernel(tc, x, w, attn_src, attn_dst, adj_t, base
         t = [held.tile([P, N], BF16, name=f"t{b}") for b in range(UB)]
         sum_cols = held.tile([P, JB], F32, name="sum_cols")
         inv_cols = held.tile([P, JB], F32, name="inv_cols")
-        inv_parts = [held.tile([P, JB], BF16, name=f"inv_part{i}") for i in range(BF16_PARTS)]
-        inv_rests = [held.tile([P, JB], F32, name=f"inv_rest{i}") for i in range(BF16_PARTS - 1)]
         inv_sum = held.tile([P, N], F32, name="inv_sum")
-        identity = held.tile([P, P], BF16, name="identity")
-        make_identity(nc, identity[:])
+        identity_bf16 = held.tile([P, P], BF16, name="identity_bf16")
+        make_identity(nc, identity_bf16[:])
+        identity_f32 = held.tile([P, P], F32, name="identity_f32")
+        make_identity(nc, identity_f32[:])
 
         with (
             tc.tile_pool(name="early", bufs=1) as early,
@@ -164,7 +162,7 @@ def tile_sparsegraphattention_b_kernel(tc, x, w, attn_src, attn_dst, adj_t, base
 
             receiver_rows = early.tile([P, N], BF16, name="receiver_rows")
             for jc in range(JC):
-                rows_ps = spread([receiver_cols], jc, f"rows_ps{jc}")
+                rows_ps = spread(receiver_cols, identity_bf16, jc, f"rows_ps{jc}")
                 if jc % 2 == 0:
                     nc.scalar.copy(receiver_rows[:, chunk(jc)], rows_ps[:])
                 else:
@@ -192,14 +190,8 @@ def tile_sparsegraphattention_b_kernel(tc, x, w, attn_src, attn_dst, adj_t, base
                 out=sum_cols[:], in_=part_sums[:, 0 : JB * UB].rearrange("p (jb b) -> p jb b", b=UB), axis=AXIS_X, op=ALU.add
             )
             nc.vector.reciprocal(inv_cols[:], sum_cols[:])
-            rest = inv_cols
-            for i in range(BF16_PARTS):
-                nc.vector.tensor_copy(inv_parts[i][:], rest[:])
-                if i < BF16_PARTS - 1:
-                    nc.vector.tensor_tensor(inv_rests[i][:], rest[:], inv_parts[i][:], ALU.subtract)
-                    rest = inv_rests[i]
             for jc in range(JC):
-                inv_ps = spread(inv_parts, jc, f"inv_ps{jc}")
+                inv_ps = spread(inv_cols, identity_f32, jc, f"inv_ps{jc}")
                 nc.scalar.copy(inv_sum[:, chunk(jc)], inv_ps[:])
 
         with tc.tile_pool(name="addends", bufs=2) as addends:

@@ -213,7 +213,8 @@ def tile_sparsegraphattention_b_kernel(tc, x, w, attn_src, attn_dst, adj_t, base
                     nc.vector.tensor_tensor(v[:, chunk(jc)], v_ps[:], inv_sum[:, chunk(jc)], ALU.mult)
                     if jc % 2 == 1:
                         nc.scalar.activation(out=exp_v[:, half(jc // 2)], in_=v[:, half(jc // 2)], func=ACT.Exp)
-                nc.vector.tensor_scalar_max(p[:], v[:], 0.0)
+                nc.vector.tensor_scalar_max(p[:, half(1)], v[:, half(1)], 0.0)
+                nc.scalar.activation(out=p[:, half(0)], in_=v[:, half(0)], func=ACT.Relu)
                 for side in range(2):
                     nc.vector.tensor_scalar(
                         out=q[:, half(side)], in0=exp_v[:, half(side)], scalar1=1.0, scalar2=-1.0,

@@ -6,7 +6,6 @@ BF16 = mybir.dt.bfloat16
 U16 = mybir.dt.uint16
 ALU = mybir.AluOpType
 ACT = mybir.ActivationFunctionType
-AXIS_X = mybir.AxisListType.X
 
 P = 128
 F, C, N, SLOTS = 512, 512, 2048, 4096
@@ -22,8 +21,10 @@ JB_PER_BANK = BANK // P
 JC = N // BANK
 UB_PER_PANEL = BANK // P
 SRC, DST = 0, 1
-CB_PER_PART = 2
-PART = CB_PER_PART * P
+REST = C - P
+WIDTH = P + 1
+JB_PER_SUM_BANK = BANK // WIDTH
+SUM_BANKS = (JB + JB_PER_SUM_BANK - 1) // JB_PER_SUM_BANK
 
 FLOPS = 2 * F * C * N + 2 * 2 * C * N + 2 * C * N * N
 
@@ -65,20 +66,14 @@ def tile_sparsegraphattention_b_kernel(tc, x, w, attn_src, attn_dst, adj_t, base
             first = (b % UB_PER_PANEL) * P
             return x_panels[b // UB_PER_PANEL][:, kb, first : first + P]
 
-        def project(part, free_bank):
-            for pair in range(UB // 2):
-                h_ps = free_bank(f"h_ps{part}_{pair}")
-                for i in range(2):
-                    b = 2 * pair + i
-                    for kb in range(KB):
-                        nc.tensor.matmul(
-                            h_ps[:, i * PART : (i + 1) * PART], lhsT=x_block(b, kb),
-                            rhs=w_sb[:, kb, part * PART : (part + 1) * PART], start=(kb == 0), stop=(kb == KB - 1),
-                        )
-                    nc.scalar.activation(
-                        out=h_t[part][b][:], in_=h_ps[:, i * PART : (i + 1) * PART], func=ACT.Copy,
-                        scale=factor[:, b : b + 1],
-                    )
+        def project(h_ps, b, first, width):
+            for kb in range(KB):
+                nc.tensor.matmul(
+                    h_ps, lhsT=x_block(b, kb), rhs=w_sb[:, kb, first : first + width], start=(kb == 0), stop=(kb == KB - 1)
+                )
+
+        def scaled(out_rows, h_ps, b):
+            nc.scalar.activation(out=out_rows, in_=h_ps, func=ACT.Copy, scale=factor[:, b : b + 1])
 
         def load_window(cb):
             window = windows.tile([P, SLOTS], F32, name="window")
@@ -86,12 +81,12 @@ def tile_sparsegraphattention_b_kernel(tc, x, w, attn_src, attn_dst, adj_t, base
             return window
 
         offsets = held.tile([P, N // 16], U16, name="offsets")
-        h_t = [[held.tile([P, PART], BF16, name=f"h_t{part}_{b}") for b in range(UB)] for part in range(C // PART)]
+        h_first = held.tile([P, UB, P + 2], BF16, name="h_first")
+        h_rest = [held.tile([P, REST], BF16, name=f"h_rest{b}") for b in range(UB)]
         w_sb = held.tile([P, KB, C], BF16, name="w_sb")
         x_panels = [held.tile([P, KB, BANK], BF16, name=f"x_panel{jc}") for jc in range(JC)]
         factor = held.tile([P, UB], F32, name="factor")
         t = [held.tile([P, N], BF16, name=f"t{b}") for b in range(UB)]
-        sum_cols = held.tile([P, JB], F32, name="sum_cols")
         inv_cols = held.tile([P, JB], F32, name="inv_cols")
         inv_sum = held.tile([P, N], F32, name="inv_sum")
         identity_bf16 = held.tile([P, P], BF16, name="identity_bf16")
@@ -157,8 +152,9 @@ def tile_sparsegraphattention_b_kernel(tc, x, w, attn_src, attn_dst, adj_t, base
                 out=sender_floor[:], in_=a_src_cols, func=ACT.Exp, bias=bias_steep[:, 0:1], scale=1.0 - SLOPE
             )
             nc.scalar.activation(out=factor[:], in_=a_src_cols, func=ACT.Exp, bias=bias_flat[:, 0:1], scale=SLOPE)
-            factor_bf16 = early.tile([P, UB], BF16, name="factor_bf16")
-            nc.scalar.activation(out=factor_bf16[:], in_=a_src_cols, func=ACT.Exp, bias=bias_flat[:, 0:1], scale=SLOPE)
+            nc.scalar.activation(
+                out=h_first[:, :, P], in_=a_src_cols, func=ACT.Exp, bias=bias_flat[:, 0:1], scale=SLOPE
+            )
 
             receiver_rows = early.tile([P, N], BF16, name="receiver_rows")
             for jc in range(JC):
@@ -168,9 +164,14 @@ def tile_sparsegraphattention_b_kernel(tc, x, w, attn_src, attn_dst, adj_t, base
                 else:
                     nc.vector.tensor_copy(receiver_rows[:, chunk(jc)], rows_ps[:])
 
-            project(0, bank)
+            for group in range(UB // JB_PER_BANK):
+                h_ps = bank(f"h_ps{group}")
+                for i in range(JB_PER_BANK):
+                    b = group * JB_PER_BANK + i
+                    project(h_ps[:, i * P : (i + 1) * P], b, 0, P)
+                    scaled(h_first[:, b, 0:P], h_ps[:, i * P : (i + 1) * P], b)
 
-            part_sums = side_bank("part_sums")
+            sum_banks = [bank(f"sum_bank{k}") for k in range(SUM_BANKS)]
             for b in range(UB):
                 adj = adjacency.tile([P, N], F32, name="adj")
                 nc.sync.dma_start(adj[:], adj_t[b * P : (b + 1) * P, :])
@@ -179,42 +180,21 @@ def tile_sparsegraphattention_b_kernel(tc, x, w, attn_src, attn_dst, adj_t, base
                     op0=ALU.max, op1=ALU.mult,
                 )
                 for jb in range(JB):
+                    k, seat = divmod(jb, JB_PER_SUM_BANK)
+                    last_in_bank = seat == JB_PER_SUM_BANK - 1 or jb == JB - 1
                     nc.tensor.matmul(
-                        part_sums[:, jb * UB + b : jb * UB + b + 1], lhsT=t[b][:, jb * P : (jb + 1) * P],
-                        rhs=factor_bf16[:, b : b + 1], start=True, stop=True,
+                        sum_banks[k][:, seat * WIDTH : (seat + 1) * WIDTH], lhsT=t[b][:, jb * P : (jb + 1) * P],
+                        rhs=h_first[:, b, 0:WIDTH], start=(b == 0 and seat == 0), stop=(b == UB - 1 and last_in_bank),
                     )
+                rest_ps = side_bank(f"rest_ps{b}")
+                project(rest_ps[:, 0:REST], b, P, REST)
+                scaled(h_rest[b][:], rest_ps[:, 0:REST], b)
 
             loaded = [load_window(0), load_window(1)]
 
-            nc.vector.tensor_reduce(
-                out=sum_cols[:], in_=part_sums[:, 0 : JB * UB].rearrange("p (jb b) -> p jb b", b=UB), axis=AXIS_X, op=ALU.add
-            )
-            nc.vector.reciprocal(inv_cols[:], sum_cols[:])
-            for jc in range(JC):
-                inv_ps = spread(inv_cols, identity_f32, jc, f"inv_ps{jc}")
-                nc.scalar.copy(inv_sum[:, chunk(jc)], inv_ps[:])
+        with tc.tile_pool(name="addends", bufs=2) as addends, tc.tile_pool(name="turned", bufs=1) as turned:
 
-        with tc.tile_pool(name="addends", bufs=2) as addends:
-            for cb in range(CB):
-                part, block = divmod(cb, CB_PER_PART)
-                if cb == CB_PER_PART - 1:
-                    project(1, side_bank)
-                v = addends.tile([P, N], F32, name="v")
-                exp_v = addends.tile([P, N], F32, name="exp_v")
-                p = addends.tile([P, N], F32, name="p")
-                q = addends.tile([P, N], F32, name="q")
-                for jc in range(JC):
-                    v_ps = bank(f"v_ps{cb}_{jc}")
-                    for b in range(UB):
-                        nc.tensor.matmul(
-                            v_ps[:], lhsT=h_t[part][b][:, block * P : (block + 1) * P], rhs=t[b][:, chunk(jc)],
-                            start=(b == 0), stop=(b == UB - 1),
-                        )
-                    nc.vector.tensor_tensor(v[:, chunk(jc)], v_ps[:], inv_sum[:, chunk(jc)], ALU.mult)
-                    if jc % 2 == 1:
-                        nc.scalar.activation(out=exp_v[:, half(jc // 2)], in_=v[:, half(jc // 2)], func=ACT.Exp)
-                nc.vector.tensor_scalar_max(p[:, half(1)], v[:, half(1)], 0.0)
-                nc.scalar.activation(out=p[:, half(0)], in_=v[:, half(0)], func=ACT.Relu)
+            def finish(cb, exp_v, p, q):
                 for side in range(2):
                     nc.vector.tensor_scalar(
                         out=q[:, half(side)], in0=exp_v[:, half(side)], scalar1=1.0, scalar2=-1.0,
@@ -224,3 +204,58 @@ def tile_sparsegraphattention_b_kernel(tc, x, w, attn_src, attn_dst, adj_t, base
                 nc.sync.dma_start(out[cb * P : (cb + 1) * P, :], loaded[cb][:])
                 if cb + 2 < CB:
                     loaded.append(load_window(cb + 2))
+
+            v_turned = turned.tile([P, JB, P], F32, name="v_turned")
+            for k in range(SUM_BANKS):
+                jbs = range(k * JB_PER_SUM_BANK, min((k + 1) * JB_PER_SUM_BANK, JB))
+                n = len(jbs)
+                inv = inv_cols[:, jbs[0] : jbs[0] + n]
+                nc.vector.reciprocal(inv, sum_banks[k][:, P : n * WIDTH : WIDTH])
+                if k % 2 == 0:
+                    nc.vector.tensor_tensor(
+                        v_turned[:, jbs[0] : jbs[0] + n, :],
+                        sum_banks[k][:, 0 : n * WIDTH].rearrange("p (j c) -> p j c", c=WIDTH)[:, :, 0:P],
+                        inv.unsqueeze(2).to_broadcast([P, n, P]), ALU.mult,
+                    )
+                else:
+                    for i, jb in enumerate(jbs):
+                        nc.scalar.activation(
+                            out=v_turned[:, jb, :], in_=sum_banks[k][:, i * WIDTH : i * WIDTH + P], func=ACT.Copy,
+                            scale=inv_cols[:, jb : jb + 1],
+                        )
+            exp_v = addends.tile([P, N], F32, name="exp_v")
+            p = addends.tile([P, N], F32, name="p")
+            q = addends.tile([P, N], F32, name="q")
+            for jc in range(JC):
+                v_ps = side_bank(f"turned_ps{jc}")
+                for i in range(JB_PER_BANK):
+                    nc.tensor.transpose(v_ps[:, i * P : (i + 1) * P], v_turned[:, jc * JB_PER_BANK + i, :], identity_f32[:])
+                nc.scalar.activation(out=exp_v[:, chunk(jc)], in_=v_ps[:], func=ACT.Exp)
+                if jc % 2 == 0:
+                    nc.scalar.activation(out=p[:, chunk(jc)], in_=v_ps[:], func=ACT.Relu)
+                else:
+                    nc.vector.tensor_scalar_max(p[:, chunk(jc)], v_ps[:], 0.0)
+            finish(0, exp_v, p, q)
+
+            for jc in range(JC):
+                inv_ps = spread(inv_cols, identity_f32, jc, f"inv_ps{jc}")
+                nc.scalar.copy(inv_sum[:, chunk(jc)], inv_ps[:])
+
+            for cb in range(1, CB):
+                v = addends.tile([P, N], F32, name="v")
+                exp_v = addends.tile([P, N], F32, name="exp_v")
+                p = addends.tile([P, N], F32, name="p")
+                q = addends.tile([P, N], F32, name="q")
+                for jc in range(JC):
+                    v_ps = bank(f"v_ps{cb}_{jc}")
+                    for b in range(UB):
+                        nc.tensor.matmul(
+                            v_ps[:], lhsT=h_rest[b][:, (cb - 1) * P : cb * P], rhs=t[b][:, chunk(jc)],
+                            start=(b == 0), stop=(b == UB - 1),
+                        )
+                    nc.vector.tensor_tensor(v[:, chunk(jc)], v_ps[:], inv_sum[:, chunk(jc)], ALU.mult)
+                    if jc % 2 == 1:
+                        nc.scalar.activation(out=exp_v[:, half(jc // 2)], in_=v[:, half(jc // 2)], func=ACT.Exp)
+                nc.vector.tensor_scalar_max(p[:, half(1)], v[:, half(1)], 0.0)
+                nc.scalar.activation(out=p[:, half(0)], in_=v[:, half(0)], func=ACT.Relu)
+                finish(cb, exp_v, p, q)

@@ -35,13 +35,12 @@ def tile_sparsegraphattention_b_kernel(tc, x, w, attn_src, attn_dst, adj_t, base
         tc.tile_pool(name="held", bufs=1) as held,
         tc.tile_pool(name="windows", bufs=2) as windows,
         tc.psum_pool(name="banks", bufs=WIDE_BANKS) as banks,
-        tc.psum_pool(name="side_banks", bufs=SIDE_BANKS) as side_banks,
     ):
-        def bank(name):
-            return banks.tile([P, BANK], F32, tag="bank", name=name)
+        def a_bank(pool, name):
+            return pool.tile([P, BANK], F32, tag="bank", name=name)
 
-        def side_bank(name):
-            return side_banks.tile([P, BANK], F32, tag="side_bank", name=name)
+        def bank(name):
+            return a_bank(banks, name)
 
         def chunk(jc):
             return slice(jc * BANK, (jc + 1) * BANK)
@@ -52,12 +51,12 @@ def tile_sparsegraphattention_b_kernel(tc, x, w, attn_src, attn_dst, adj_t, base
         def repeated(column):
             return column.to_broadcast([P, P])
 
-        def spread(cols, identity, jc, name):
-            row_ps = side_bank(name)
+        def spread(pool, cols, jc, name):
+            row_ps = a_bank(pool, name)
             for k in range(JB_PER_BANK):
                 jb = jc * JB_PER_BANK + k
                 nc.tensor.matmul(
-                    row_ps[:, k * P : (k + 1) * P], lhsT=repeated(cols[:, jb : jb + 1]), rhs=identity[:],
+                    row_ps[:, k * P : (k + 1) * P], lhsT=repeated(cols[:, jb : jb + 1]), rhs=identity_bf16[:],
                     start=True, stop=True,
                 )
             return row_ps
@@ -123,46 +122,47 @@ def tile_sparsegraphattention_b_kernel(tc, x, w, attn_src, attn_dst, adj_t, base
             w_attn = early.tile([P, KB, 2], BF16, name="w_attn")
             nc.vector.tensor_copy(w_attn[:], w_attn_f32[:])
 
-            scores_ps = side_bank("scores_ps")
-            for b in range(UB):
+            with tc.psum_pool(name="score_banks", bufs=SIDE_BANKS) as score_banks:
+                scores_ps = a_bank(score_banks, "scores_ps")
+                for b in range(UB):
+                    for kb in range(KB):
+                        nc.tensor.matmul(
+                            scores_ps[:, 2 * b : 2 * b + 2], lhsT=x_block(b, kb), rhs=w_attn[:, kb, :],
+                            start=(kb == 0), stop=(kb == KB - 1),
+                        )
                 for kb in range(KB):
                     nc.tensor.matmul(
-                        scores_ps[:, 2 * b : 2 * b + 2], lhsT=x_block(b, kb), rhs=w_attn[:, kb, :],
-                        start=(kb == 0), stop=(kb == KB - 1),
+                        scores_ps[:, 2 * UB : 2 * UB + 1], lhsT=repeated(w_attn[:, kb, DST : DST + 1]),
+                        rhs=x_panels[0][:, kb, 0:1], start=(kb == 0), stop=(kb == KB - 1),
                     )
-            for kb in range(KB):
-                nc.tensor.matmul(
-                    scores_ps[:, 2 * UB : 2 * UB + 1], lhsT=repeated(w_attn[:, kb, DST : DST + 1]),
-                    rhs=x_panels[0][:, kb, 0:1], start=(kb == 0), stop=(kb == KB - 1),
+                a_src_cols = scores_ps[:, SRC : 2 * UB : 2]
+                a_dst_cols = scores_ps[:, DST : 2 * UB : 2]
+                a_dst_0 = scores_ps[:, 2 * UB : 2 * UB + 1]
+
+                bias_steep = early.tile([P, 1], F32, name="bias_steep")
+                nc.vector.tensor_scalar_mul(bias_steep[:], a_dst_0, 1.0 - SLOPE)
+                bias_flat = early.tile([P, 1], F32, name="bias_flat")
+                nc.vector.tensor_scalar_mul(bias_flat[:], a_dst_0, SLOPE)
+                receiver_cols = early.tile([P, JB], BF16, name="receiver_cols")
+                nc.scalar.activation(
+                    out=receiver_cols[:], in_=a_dst_cols, func=ACT.Exp, bias=bias_steep[:, 0:1], scale=SLOPE - 1.0
                 )
-            a_src_cols = scores_ps[:, SRC : 2 * UB : 2]
-            a_dst_cols = scores_ps[:, DST : 2 * UB : 2]
-            a_dst_0 = scores_ps[:, 2 * UB : 2 * UB + 1]
+                sender_floor = early.tile([P, UB], F32, name="sender_floor")
+                nc.scalar.activation(
+                    out=sender_floor[:], in_=a_src_cols, func=ACT.Exp, bias=bias_steep[:, 0:1], scale=1.0 - SLOPE
+                )
+                nc.scalar.activation(out=factor[:], in_=a_src_cols, func=ACT.Exp, bias=bias_flat[:, 0:1], scale=SLOPE)
+                nc.scalar.activation(
+                    out=h_first[:, :, P], in_=a_src_cols, func=ACT.Exp, bias=bias_flat[:, 0:1], scale=SLOPE
+                )
 
-            bias_steep = early.tile([P, 1], F32, name="bias_steep")
-            nc.vector.tensor_scalar_mul(bias_steep[:], a_dst_0, 1.0 - SLOPE)
-            bias_flat = early.tile([P, 1], F32, name="bias_flat")
-            nc.vector.tensor_scalar_mul(bias_flat[:], a_dst_0, SLOPE)
-            receiver_cols = early.tile([P, JB], BF16, name="receiver_cols")
-            nc.scalar.activation(
-                out=receiver_cols[:], in_=a_dst_cols, func=ACT.Exp, bias=bias_steep[:, 0:1], scale=SLOPE - 1.0
-            )
-            sender_floor = early.tile([P, UB], F32, name="sender_floor")
-            nc.scalar.activation(
-                out=sender_floor[:], in_=a_src_cols, func=ACT.Exp, bias=bias_steep[:, 0:1], scale=1.0 - SLOPE
-            )
-            nc.scalar.activation(out=factor[:], in_=a_src_cols, func=ACT.Exp, bias=bias_flat[:, 0:1], scale=SLOPE)
-            nc.scalar.activation(
-                out=h_first[:, :, P], in_=a_src_cols, func=ACT.Exp, bias=bias_flat[:, 0:1], scale=SLOPE
-            )
-
-            receiver_rows = early.tile([P, N], BF16, name="receiver_rows")
-            for jc in range(JC):
-                rows_ps = spread(receiver_cols, identity_bf16, jc, f"rows_ps{jc}")
-                if jc % 2 == 0:
-                    nc.scalar.copy(receiver_rows[:, chunk(jc)], rows_ps[:])
-                else:
-                    nc.vector.tensor_copy(receiver_rows[:, chunk(jc)], rows_ps[:])
+                receiver_rows = early.tile([P, N], BF16, name="receiver_rows")
+                for jc in range(JC):
+                    rows_ps = spread(score_banks, receiver_cols, jc, f"rows_ps{jc}")
+                    if jc % 2 == 0:
+                        nc.scalar.copy(receiver_rows[:, chunk(jc)], rows_ps[:])
+                    else:
+                        nc.vector.tensor_copy(receiver_rows[:, chunk(jc)], rows_ps[:])
 
             for group in range(UB // JB_PER_BANK):
                 h_ps = bank(f"h_ps{group}")
@@ -172,32 +172,37 @@ def tile_sparsegraphattention_b_kernel(tc, x, w, attn_src, attn_dst, adj_t, base
                     scaled(h_first[:, b, 0:P], h_ps[:, i * P : (i + 1) * P], b)
 
             sum_banks = [bank(f"sum_bank{k}") for k in range(SUM_BANKS)]
-            for b in range(UB):
-                adj = adjacency.tile([P, N], F32, name="adj")
-                nc.sync.dma_start(adj[:], adj_t[b * P : (b + 1) * P, :])
-                nc.vector.scalar_tensor_tensor(
-                    out=t[b][:], in0=receiver_rows[:], scalar=sender_floor[:, b : b + 1], in1=adj[:],
-                    op0=ALU.max, op1=ALU.mult,
-                )
-                for jb in range(JB):
-                    k, seat = divmod(jb, JB_PER_SUM_BANK)
-                    last_in_bank = seat == JB_PER_SUM_BANK - 1 or jb == JB - 1
-                    nc.tensor.matmul(
-                        sum_banks[k][:, seat * WIDTH : (seat + 1) * WIDTH], lhsT=t[b][:, jb * P : (jb + 1) * P],
-                        rhs=h_first[:, b, 0:WIDTH], start=(b == 0 and seat == 0), stop=(b == UB - 1 and last_in_bank),
+            with tc.psum_pool(name="rest_banks", bufs=SIDE_BANKS) as rest_banks:
+                for b in range(UB):
+                    adj = adjacency.tile([P, N], F32, name="adj")
+                    nc.sync.dma_start(adj[:], adj_t[b * P : (b + 1) * P, :])
+                    nc.vector.scalar_tensor_tensor(
+                        out=t[b][:], in0=receiver_rows[:], scalar=sender_floor[:, b : b + 1], in1=adj[:],
+                        op0=ALU.max, op1=ALU.mult,
                     )
-                rest_ps = side_bank(f"rest_ps{b}")
-                project(rest_ps[:, 0:REST], b, P, REST)
-                scaled(h_rest[b][:], rest_ps[:, 0:REST], b)
+                    for jb in range(JB):
+                        k, seat = divmod(jb, JB_PER_SUM_BANK)
+                        last_in_bank = seat == JB_PER_SUM_BANK - 1 or jb == JB - 1
+                        nc.tensor.matmul(
+                            sum_banks[k][:, seat * WIDTH : (seat + 1) * WIDTH], lhsT=t[b][:, jb * P : (jb + 1) * P],
+                            rhs=h_first[:, b, 0:WIDTH], start=(b == 0 and seat == 0), stop=(b == UB - 1 and last_in_bank),
+                        )
+                    rest_ps = a_bank(rest_banks, f"rest_ps{b}")
+                    project(rest_ps[:, 0:REST], b, P, REST)
+                    scaled(h_rest[b][:], rest_ps[:, 0:REST], b)
 
             loaded = [load_window(0), load_window(1)]
 
-        with tc.tile_pool(name="addends", bufs=2) as addends, tc.tile_pool(name="turned", bufs=1) as turned:
+        with (
+            tc.tile_pool(name="addends", bufs=2) as addends,
+            tc.tile_pool(name="turned", bufs=1) as turned,
+            tc.psum_pool(name="turn_banks", bufs=SIDE_BANKS) as turn_banks,
+        ):
 
             def finish(cb, exp_v, p, q):
-                for side in range(2):
+                for jc in range(JC):
                     nc.vector.tensor_scalar(
-                        out=q[:, half(side)], in0=exp_v[:, half(side)], scalar1=1.0, scalar2=-1.0,
+                        out=q[:, chunk(jc)], in0=exp_v[:, chunk(jc)], scalar1=1.0, scalar2=-1.0,
                         op0=ALU.min, op1=ALU.add,
                     )
                 nc.vector.tensor_tensor(loaded[cb][:].indirect(offsets[:]), p[:], q[:], ALU.add)
@@ -225,9 +230,9 @@ def tile_sparsegraphattention_b_kernel(tc, x, w, attn_src, attn_dst, adj_t, base
                         )
             exp_v = addends.tile([P, N], F32, name="exp_v")
             p = addends.tile([P, N], F32, name="p")
-            q = addends.tile([P, N], F32, name="q")
+            q = addends.tile([P, N], F32, name="v")
             for jc in range(JC):
-                v_ps = side_bank(f"turned_ps{jc}")
+                v_ps = a_bank(turn_banks, f"turned_ps{jc}")
                 for i in range(JB_PER_BANK):
                     nc.tensor.transpose(v_ps[:, i * P : (i + 1) * P], v_turned[:, jc * JB_PER_BANK + i, :], identity_f32[:])
                 nc.scalar.activation(out=exp_v[:, chunk(jc)], in_=v_ps[:], func=ACT.Exp)
@@ -237,15 +242,19 @@ def tile_sparsegraphattention_b_kernel(tc, x, w, attn_src, attn_dst, adj_t, base
                     nc.vector.tensor_scalar_max(p[:, chunk(jc)], v_ps[:], 0.0)
             finish(0, exp_v, p, q)
 
-            for jc in range(JC):
-                inv_ps = spread(inv_cols, identity_f32, jc, f"inv_ps{jc}")
-                nc.scalar.copy(inv_sum[:, chunk(jc)], inv_ps[:])
+            inv_ps = a_bank(turn_banks, "inv_ps")
+            nc.tensor.transpose(inv_ps[0:JB, 0:P], inv_cols[:], identity_f32[:])
+            inv_rows = turned.tile([P, P], F32, name="inv_rows")
+            nc.vector.tensor_copy(inv_rows[0:JB, :], inv_ps[0:JB, 0:P])
+            parked = out[C - 1 : C, 0:N]
+            nc.sync.dma_start(parked.rearrange("one (jb p) -> (one jb) p", p=P), inv_rows[0:JB, :])
+            nc.sync.dma_start(inv_sum[:], parked.rearrange("one j -> (one j)").partition_broadcast(P))
 
             for cb in range(1, CB):
                 v = addends.tile([P, N], F32, name="v")
                 exp_v = addends.tile([P, N], F32, name="exp_v")
                 p = addends.tile([P, N], F32, name="p")
-                q = addends.tile([P, N], F32, name="q")
+                q = v
                 for jc in range(JC):
                     v_ps = bank(f"v_ps{cb}_{jc}")
                     for b in range(UB):
@@ -254,8 +263,6 @@ def tile_sparsegraphattention_b_kernel(tc, x, w, attn_src, attn_dst, adj_t, base
                             start=(b == 0), stop=(b == UB - 1),
                         )
                     nc.vector.tensor_tensor(v[:, chunk(jc)], v_ps[:], inv_sum[:, chunk(jc)], ALU.mult)
-                    if jc % 2 == 1:
-                        nc.scalar.activation(out=exp_v[:, half(jc // 2)], in_=v[:, half(jc // 2)], func=ACT.Exp)
-                nc.vector.tensor_scalar_max(p[:, half(1)], v[:, half(1)], 0.0)
-                nc.scalar.activation(out=p[:, half(0)], in_=v[:, half(0)], func=ACT.Relu)
+                    nc.scalar.activation(out=exp_v[:, chunk(jc)], in_=v[:, chunk(jc)], func=ACT.Exp)
+                nc.vector.tensor_scalar_max(p[:], v[:], 0.0)
                 finish(cb, exp_v, p, q)

@@ -20,11 +20,10 @@ JB = N // P
 JB_PER_BANK = BANK // P
 JC = N // BANK
 UB_PER_PANEL = BANK // P
-SRC, DST = 0, 1
 REST = C - P
 WIDTH = P + 1
-JB_PER_SUM_BANK = BANK // WIDTH
-SUM_BANKS = (JB + JB_PER_SUM_BANK - 1) // JB_PER_SUM_BANK
+BLOCKS_PER_BANK = BANK // WIDTH
+SUM_BANKS = (JB + BLOCKS_PER_BANK - 1) // BLOCKS_PER_BANK
 
 FLOPS = 2 * F * C * N + 2 * 2 * C * N + 2 * C * N * N
 
@@ -35,12 +34,13 @@ def tile_sparsegraphattention_b_kernel(tc, x, w, attn_src, attn_dst, adj_t, base
         tc.tile_pool(name="held", bufs=1) as held,
         tc.tile_pool(name="windows", bufs=2) as windows,
         tc.psum_pool(name="banks", bufs=WIDE_BANKS) as banks,
+        tc.psum_pool(name="side_banks", bufs=SIDE_BANKS) as side_banks,
     ):
-        def a_bank(pool, name):
-            return pool.tile([P, BANK], F32, tag="bank", name=name)
-
         def bank(name):
-            return a_bank(banks, name)
+            return banks.tile([P, BANK], F32, tag="bank", name=name)
+
+        def side_bank(name):
+            return side_banks.tile([P, BANK], F32, tag="side_bank", name=name)
 
         def chunk(jc):
             return slice(jc * BANK, (jc + 1) * BANK)
@@ -51,25 +51,13 @@ def tile_sparsegraphattention_b_kernel(tc, x, w, attn_src, attn_dst, adj_t, base
         def repeated(column):
             return column.to_broadcast([P, P])
 
-        def spread(pool, cols, jc, name):
-            row_ps = a_bank(pool, name)
-            for k in range(JB_PER_BANK):
-                jb = jc * JB_PER_BANK + k
-                nc.tensor.matmul(
-                    row_ps[:, k * P : (k + 1) * P], lhsT=repeated(cols[:, jb : jb + 1]), rhs=identity_bf16[:],
-                    start=True, stop=True,
-                )
-            return row_ps
-
         def x_block(b, kb):
             first = (b % UB_PER_PANEL) * P
             return x_panels[b // UB_PER_PANEL][:, kb, first : first + P]
 
-        def project(h_ps, b, first, width):
+        def project(h_ps, b, w_part):
             for kb in range(KB):
-                nc.tensor.matmul(
-                    h_ps, lhsT=x_block(b, kb), rhs=w_sb[:, kb, first : first + width], start=(kb == 0), stop=(kb == KB - 1)
-                )
+                nc.tensor.matmul(h_ps, lhsT=x_block(b, kb), rhs=w_part[:, kb, :], start=(kb == 0), stop=(kb == KB - 1))
 
         def scaled(out_rows, h_ps, b):
             nc.scalar.activation(out=out_rows, in_=h_ps, func=ACT.Copy, scale=factor[:, b : b + 1])
@@ -88,8 +76,6 @@ def tile_sparsegraphattention_b_kernel(tc, x, w, attn_src, attn_dst, adj_t, base
         t = [held.tile([P, N], BF16, name=f"t{b}") for b in range(UB)]
         inv_cols = held.tile([P, JB], F32, name="inv_cols")
         inv_sum = held.tile([P, N], F32, name="inv_sum")
-        identity_bf16 = held.tile([P, P], BF16, name="identity_bf16")
-        make_identity(nc, identity_bf16[:])
         identity_f32 = held.tile([P, P], F32, name="identity_f32")
         make_identity(nc, identity_f32[:])
 
@@ -111,92 +97,85 @@ def tile_sparsegraphattention_b_kernel(tc, x, w, attn_src, attn_dst, adj_t, base
                 nc.sync.dma_start(x_panels[jc][:], x[:, chunk(jc)].rearrange("(kb p) u -> p kb u", p=P))
             nc.sync.dma_start(offsets[:], offs)
 
-            w_attn_f32 = early.tile([P, KB, 2], F32, name="w_attn_f32")
-            for place, rows in ((DST, attn_dst_rows), (SRC, attn_src_rows)):
+            def times_w(rows, rounded, name):
+                summed = early.tile([P, KB], F32, name=f"{name}_f32")
                 for kb in range(KB):
                     products = scratch.tile([P, C], F32, name="products")
                     nc.vector.scalar_tensor_tensor(
                         out=products[:], in0=w_sb[:, kb, :], scalar=1.0, in1=rows[:],
-                        op0=ALU.mult, op1=ALU.mult, accum_out=w_attn_f32[:, kb, place : place + 1],
+                        op0=ALU.mult, op1=ALU.mult, accum_out=summed[:, kb : kb + 1],
                     )
-            w_attn = early.tile([P, KB, 2], BF16, name="w_attn")
-            nc.vector.tensor_copy(w_attn[:], w_attn_f32[:])
+                nc.vector.tensor_copy(rounded, summed[:])
 
-            with tc.psum_pool(name="score_banks", bufs=SIDE_BANKS) as score_banks:
-                scores_ps = a_bank(score_banks, "scores_ps")
-                for b in range(UB):
-                    for kb in range(KB):
-                        nc.tensor.matmul(
-                            scores_ps[:, 2 * b : 2 * b + 2], lhsT=x_block(b, kb), rhs=w_attn[:, kb, :],
-                            start=(kb == 0), stop=(kb == KB - 1),
-                        )
+            w_attn_dst = early.tile([P, KB], BF16, name="w_attn_dst")
+            times_w(attn_dst_rows, w_attn_dst[:], "w_attn_dst")
+            w_first = early.tile([P, KB, P + 2], BF16, name="w_first")
+            nc.scalar.copy(w_first[:, :, 0:P], w_sb[:, :, 0:P])
+            times_w(attn_src_rows, w_first[:, :, P], "w_attn_src")
+
+            bias_steep = early.tile([P, 1], F32, name="bias_steep")
+            bias_flat = early.tile([P, 1], F32, name="bias_flat")
+            receiver_rows = early.tile([P, N], BF16, name="receiver_rows")
+            for jc in range(JC):
+                a_dst_ps = bank(f"a_dst_ps{jc}")
                 for kb in range(KB):
                     nc.tensor.matmul(
-                        scores_ps[:, 2 * UB : 2 * UB + 1], lhsT=repeated(w_attn[:, kb, DST : DST + 1]),
-                        rhs=x_panels[0][:, kb, 0:1], start=(kb == 0), stop=(kb == KB - 1),
+                        a_dst_ps[:], lhsT=repeated(w_attn_dst[:, kb : kb + 1]), rhs=x_panels[jc][:, kb, :],
+                        start=(kb == 0), stop=(kb == KB - 1),
                     )
-                a_src_cols = scores_ps[:, SRC : 2 * UB : 2]
-                a_dst_cols = scores_ps[:, DST : 2 * UB : 2]
-                a_dst_0 = scores_ps[:, 2 * UB : 2 * UB + 1]
-
-                bias_steep = early.tile([P, 1], F32, name="bias_steep")
-                nc.vector.tensor_scalar_mul(bias_steep[:], a_dst_0, 1.0 - SLOPE)
-                bias_flat = early.tile([P, 1], F32, name="bias_flat")
-                nc.vector.tensor_scalar_mul(bias_flat[:], a_dst_0, SLOPE)
-                receiver_cols = early.tile([P, JB], BF16, name="receiver_cols")
+                if jc == 0:
+                    nc.vector.tensor_scalar_mul(bias_steep[:], a_dst_ps[:, 0:1], 1.0 - SLOPE)
+                    nc.vector.tensor_scalar_mul(bias_flat[:], a_dst_ps[:, 0:1], SLOPE)
                 nc.scalar.activation(
-                    out=receiver_cols[:], in_=a_dst_cols, func=ACT.Exp, bias=bias_steep[:, 0:1], scale=SLOPE - 1.0
-                )
-                sender_floor = early.tile([P, UB], F32, name="sender_floor")
-                nc.scalar.activation(
-                    out=sender_floor[:], in_=a_src_cols, func=ACT.Exp, bias=bias_steep[:, 0:1], scale=1.0 - SLOPE
-                )
-                nc.scalar.activation(out=factor[:], in_=a_src_cols, func=ACT.Exp, bias=bias_flat[:, 0:1], scale=SLOPE)
-                nc.scalar.activation(
-                    out=h_first[:, :, P], in_=a_src_cols, func=ACT.Exp, bias=bias_flat[:, 0:1], scale=SLOPE
+                    out=receiver_rows[:, chunk(jc)], in_=a_dst_ps[:], func=ACT.Exp, bias=bias_steep[:, 0:1],
+                    scale=SLOPE - 1.0,
                 )
 
-                receiver_rows = early.tile([P, N], BF16, name="receiver_rows")
-                for jc in range(JC):
-                    rows_ps = spread(score_banks, receiver_cols, jc, f"rows_ps{jc}")
-                    if jc % 2 == 0:
-                        nc.scalar.copy(receiver_rows[:, chunk(jc)], rows_ps[:])
-                    else:
-                        nc.vector.tensor_copy(receiver_rows[:, chunk(jc)], rows_ps[:])
-
-            for group in range(UB // JB_PER_BANK):
-                h_ps = bank(f"h_ps{group}")
-                for i in range(JB_PER_BANK):
-                    b = group * JB_PER_BANK + i
-                    project(h_ps[:, i * P : (i + 1) * P], b, 0, P)
-                    scaled(h_first[:, b, 0:P], h_ps[:, i * P : (i + 1) * P], b)
+            sender_floor = early.tile([P, UB], F32, name="sender_floor")
+            for k in range(SUM_BANKS):
+                blocks = slice(k * BLOCKS_PER_BANK, min((k + 1) * BLOCKS_PER_BANK, UB))
+                n = blocks.stop - blocks.start
+                h_ps = bank(f"h_ps{k}")
+                for i in range(n):
+                    project(h_ps[:, i * WIDTH : (i + 1) * WIDTH], blocks.start + i, w_first[:, :, 0:WIDTH])
+                a_src_cols = h_ps[:, P : n * WIDTH : WIDTH]
+                nc.scalar.activation(
+                    out=sender_floor[:, blocks], in_=a_src_cols, func=ACT.Exp, bias=bias_steep[:, 0:1], scale=1.0 - SLOPE
+                )
+                nc.scalar.activation(
+                    out=factor[:, blocks], in_=a_src_cols, func=ACT.Exp, bias=bias_flat[:, 0:1], scale=SLOPE
+                )
+                nc.scalar.activation(
+                    out=h_first[:, blocks, P], in_=a_src_cols, func=ACT.Exp, bias=bias_flat[:, 0:1], scale=SLOPE
+                )
+                for i in range(n):
+                    b = blocks.start + i
+                    scaled(h_first[:, b, 0:P], h_ps[:, i * WIDTH : i * WIDTH + P], b)
 
             sum_banks = [bank(f"sum_bank{k}") for k in range(SUM_BANKS)]
-            with tc.psum_pool(name="rest_banks", bufs=SIDE_BANKS) as rest_banks:
-                for b in range(UB):
-                    adj = adjacency.tile([P, N], F32, name="adj")
-                    nc.sync.dma_start(adj[:], adj_t[b * P : (b + 1) * P, :])
-                    nc.vector.scalar_tensor_tensor(
-                        out=t[b][:], in0=receiver_rows[:], scalar=sender_floor[:, b : b + 1], in1=adj[:],
-                        op0=ALU.max, op1=ALU.mult,
+            for b in range(UB):
+                adj = adjacency.tile([P, N], F32, name="adj")
+                nc.sync.dma_start(adj[:], adj_t[b * P : (b + 1) * P, :])
+                nc.vector.scalar_tensor_tensor(
+                    out=t[b][:], in0=receiver_rows[:], scalar=sender_floor[:, b : b + 1], in1=adj[:],
+                    op0=ALU.max, op1=ALU.mult,
+                )
+                for jb in range(JB):
+                    k, seat = divmod(jb, BLOCKS_PER_BANK)
+                    last_in_bank = seat == BLOCKS_PER_BANK - 1 or jb == JB - 1
+                    nc.tensor.matmul(
+                        sum_banks[k][:, seat * WIDTH : (seat + 1) * WIDTH], lhsT=t[b][:, jb * P : (jb + 1) * P],
+                        rhs=h_first[:, b, 0:WIDTH], start=(b == 0 and seat == 0), stop=(b == UB - 1 and last_in_bank),
                     )
-                    for jb in range(JB):
-                        k, seat = divmod(jb, JB_PER_SUM_BANK)
-                        last_in_bank = seat == JB_PER_SUM_BANK - 1 or jb == JB - 1
-                        nc.tensor.matmul(
-                            sum_banks[k][:, seat * WIDTH : (seat + 1) * WIDTH], lhsT=t[b][:, jb * P : (jb + 1) * P],
-                            rhs=h_first[:, b, 0:WIDTH], start=(b == 0 and seat == 0), stop=(b == UB - 1 and last_in_bank),
-                        )
-                    rest_ps = a_bank(rest_banks, f"rest_ps{b}")
-                    project(rest_ps[:, 0:REST], b, P, REST)
-                    scaled(h_rest[b][:], rest_ps[:, 0:REST], b)
+                rest_ps = side_bank(f"rest_ps{b}")
+                project(rest_ps[:, 0:REST], b, w_sb[:, :, P:C])
+                scaled(h_rest[b][:], rest_ps[:, 0:REST], b)
 
             loaded = [load_window(0), load_window(1)]
 
         with (
             tc.tile_pool(name="addends", bufs=2) as addends,
             tc.tile_pool(name="turned", bufs=1) as turned,
-            tc.psum_pool(name="turn_banks", bufs=SIDE_BANKS) as turn_banks,
         ):
 
             def finish(cb, exp_v, p, q):
@@ -212,7 +191,7 @@ def tile_sparsegraphattention_b_kernel(tc, x, w, attn_src, attn_dst, adj_t, base
 
             v_turned = turned.tile([P, JB, P], F32, name="v_turned")
             for k in range(SUM_BANKS):
-                jbs = range(k * JB_PER_SUM_BANK, min((k + 1) * JB_PER_SUM_BANK, JB))
+                jbs = range(k * BLOCKS_PER_BANK, min((k + 1) * BLOCKS_PER_BANK, JB))
                 n = len(jbs)
                 inv = inv_cols[:, jbs[0] : jbs[0] + n]
                 nc.vector.reciprocal(inv, sum_banks[k][:, P : n * WIDTH : WIDTH])
@@ -232,7 +211,7 @@ def tile_sparsegraphattention_b_kernel(tc, x, w, attn_src, attn_dst, adj_t, base
             p = addends.tile([P, N], F32, name="p")
             q = addends.tile([P, N], F32, name="v")
             for jc in range(JC):
-                v_ps = a_bank(turn_banks, f"turned_ps{jc}")
+                v_ps = bank(f"turned_ps{jc}")
                 for i in range(JB_PER_BANK):
                     nc.tensor.transpose(v_ps[:, i * P : (i + 1) * P], v_turned[:, jc * JB_PER_BANK + i, :], identity_f32[:])
                 nc.scalar.activation(out=exp_v[:, chunk(jc)], in_=v_ps[:], func=ACT.Exp)
@@ -242,7 +221,7 @@ def tile_sparsegraphattention_b_kernel(tc, x, w, attn_src, attn_dst, adj_t, base
                     nc.vector.tensor_scalar_max(p[:, chunk(jc)], v_ps[:], 0.0)
             finish(0, exp_v, p, q)
 
-            inv_ps = a_bank(turn_banks, "inv_ps")
+            inv_ps = bank("inv_ps")
             nc.tensor.transpose(inv_ps[0:JB, 0:P], inv_cols[:], identity_f32[:])
             inv_rows = turned.tile([P, P], F32, name="inv_rows")
             nc.vector.tensor_copy(inv_rows[0:JB, :], inv_ps[0:JB, 0:P])
@@ -256,11 +235,11 @@ def tile_sparsegraphattention_b_kernel(tc, x, w, attn_src, attn_dst, adj_t, base
                 p = addends.tile([P, N], F32, name="p")
                 q = v
                 for jc in range(JC):
-                    v_ps = bank(f"v_ps{cb}_{jc}")
-                    for b in range(UB):
+                    v_ps = (side_bank if cb == 1 and jc < SIDE_BANKS else bank)(f"v_ps{cb}_{jc}")
+                    for b in reversed(range(UB)):
                         nc.tensor.matmul(
                             v_ps[:], lhsT=h_rest[b][:, (cb - 1) * P : cb * P], rhs=t[b][:, chunk(jc)],
-                            start=(b == 0), stop=(b == UB - 1),
+                            start=(b == UB - 1), stop=(b == 0),
                         )
                     nc.vector.tensor_tensor(v[:, chunk(jc)], v_ps[:], inv_sum[:, chunk(jc)], ALU.mult)
                     nc.scalar.activation(out=exp_v[:, chunk(jc)], in_=v[:, chunk(jc)], func=ACT.Exp)

@@ -24,6 +24,7 @@ REST = C - P
 WIDTH = P + 1
 BLOCKS_PER_BANK = BANK // WIDTH
 SUM_BANKS = (JB + BLOCKS_PER_BANK - 1) // BLOCKS_PER_BANK
+HALVED_BLOCKS = 2
 
 FLOPS = 2 * F * C * N + 2 * 2 * C * N + 2 * C * N * N
 
@@ -124,8 +125,8 @@ def tile_sparsegraphattention_b_kernel(tc, x, w, attn_src, attn_dst, adj_t, base
                         start=(kb == 0), stop=(kb == KB - 1),
                     )
                 if jc == 0:
-                    nc.vector.tensor_scalar_mul(bias_steep[:], a_dst_ps[:, 0:1], 1.0 - SLOPE)
-                    nc.vector.tensor_scalar_mul(bias_flat[:], a_dst_ps[:, 0:1], SLOPE)
+                    nc.scalar.mul(bias_steep[:], a_dst_ps[:, 0:1], 1.0 - SLOPE)
+                    nc.scalar.mul(bias_flat[:], a_dst_ps[:, 0:1], SLOPE)
                 nc.scalar.activation(
                     out=receiver_rows[:, chunk(jc)], in_=a_dst_ps[:], func=ACT.Exp, bias=bias_steep[:, 0:1],
                     scale=SLOPE - 1.0,
@@ -153,23 +154,37 @@ def tile_sparsegraphattention_b_kernel(tc, x, w, attn_src, attn_dst, adj_t, base
                     scaled(h_first[:, b, 0:P], h_ps[:, i * WIDTH : i * WIDTH + P], b)
 
             sum_banks = [bank(f"sum_bank{k}") for k in range(SUM_BANKS)]
-            for b in range(UB):
-                adj = adjacency.tile([P, N], F32, name="adj")
-                nc.sync.dma_start(adj[:], adj_t[b * P : (b + 1) * P, :])
+            def make_t(b, adj, receivers):
                 nc.vector.scalar_tensor_tensor(
-                    out=t[b][:], in0=receiver_rows[:], scalar=sender_floor[:, b : b + 1], in1=adj[:],
-                    op0=ALU.max, op1=ALU.mult,
+                    out=t[b][:, receivers], in0=receiver_rows[:, receivers], scalar=sender_floor[:, b : b + 1],
+                    in1=adj[:, receivers], op0=ALU.max, op1=ALU.mult,
                 )
-                for jb in range(JB):
+
+            def aggregate_first(b, jbs):
+                for jb in jbs:
                     k, seat = divmod(jb, BLOCKS_PER_BANK)
                     last_in_bank = seat == BLOCKS_PER_BANK - 1 or jb == JB - 1
                     nc.tensor.matmul(
                         sum_banks[k][:, seat * WIDTH : (seat + 1) * WIDTH], lhsT=t[b][:, jb * P : (jb + 1) * P],
                         rhs=h_first[:, b, 0:WIDTH], start=(b == 0 and seat == 0), stop=(b == UB - 1 and last_in_bank),
                     )
+
+            last_adj = {}
+            for b in range(UB):
+                adj = adjacency.tile([P, N], F32, name="adj")
+                nc.sync.dma_start(adj[:], adj_t[b * P : (b + 1) * P, :])
+                if b < UB - HALVED_BLOCKS:
+                    make_t(b, adj, slice(0, N))
+                    aggregate_first(b, range(JB))
+                else:
+                    last_adj[b] = adj
                 rest_ps = side_bank(f"rest_ps{b}")
                 project(rest_ps[:, 0:REST], b, w_sb[:, :, P:C])
                 scaled(h_rest[b][:], rest_ps[:, 0:REST], b)
+            for side in range(2):
+                for b, adj in last_adj.items():
+                    make_t(b, adj, half(side))
+                    aggregate_first(b, range(side * JB // 2, (side + 1) * JB // 2))
 
             loaded = [load_window(0), load_window(1)]
 
@@ -179,9 +194,9 @@ def tile_sparsegraphattention_b_kernel(tc, x, w, attn_src, attn_dst, adj_t, base
         ):
 
             def finish(cb, exp_v, p, q):
-                for jc in range(JC):
+                for part in (half(0), chunk(2), chunk(3)):
                     nc.vector.tensor_scalar(
-                        out=q[:, chunk(jc)], in0=exp_v[:, chunk(jc)], scalar1=1.0, scalar2=-1.0,
+                        out=q[:, part], in0=exp_v[:, part], scalar1=1.0, scalar2=-1.0,
                         op0=ALU.min, op1=ALU.add,
                     )
                 nc.vector.tensor_tensor(loaded[cb][:].indirect(offsets[:]), p[:], q[:], ALU.add)
@@ -243,5 +258,6 @@ def tile_sparsegraphattention_b_kernel(tc, x, w, attn_src, attn_dst, adj_t, base
                         )
                     nc.vector.tensor_tensor(v[:, chunk(jc)], v_ps[:], inv_sum[:, chunk(jc)], ALU.mult)
                     nc.scalar.activation(out=exp_v[:, chunk(jc)], in_=v[:, chunk(jc)], func=ACT.Exp)
-                nc.vector.tensor_scalar_max(p[:], v[:], 0.0)
+                nc.scalar.activation(out=p[:, chunk(0)], in_=v[:, chunk(0)], func=ACT.Relu)
+                nc.vector.tensor_scalar_max(p[:, BANK:N], v[:, BANK:N], 0.0)
                 finish(cb, exp_v, p, q)

import concourse.mybir as mybir
from concourse.masks import make_identity

F32 = mybir.dt.float32
BF16 = mybir.dt.bfloat16
U16 = mybir.dt.uint16
ALU = mybir.AluOpType
ACT = mybir.ActivationFunctionType

P = 128
F, C, N, SLOTS = 512, 512, 2048, 4096
SLOPE = 0.2
BANK = 512
WIDE_BANKS = 6
SIDE_BANKS = 2
KB = F // P
CB = C // P
UB = N // P
JB = N // P
JB_PER_BANK = BANK // P
JC = N // BANK
UB_PER_PANEL = BANK // P
REST = C - P
WIDTH = P + 1
BLOCKS_PER_BANK = BANK // WIDTH
SUM_BANKS = (JB + BLOCKS_PER_BANK - 1) // BLOCKS_PER_BANK
HALVED_BLOCKS = 2

FLOPS = 2 * F * C * N + 2 * 2 * C * N + 2 * C * N * N


def tile_sparsegraphattention_b_kernel(tc, x, w, attn_src, attn_dst, adj_t, base, offs, out):
    nc = tc.nc
    with (
        tc.tile_pool(name="held", bufs=1) as held,
        tc.tile_pool(name="windows", bufs=2) as windows,
        tc.psum_pool(name="banks", bufs=WIDE_BANKS) as banks,
        tc.psum_pool(name="side_banks", bufs=SIDE_BANKS) as side_banks,
    ):
        def bank(name):
            return banks.tile([P, BANK], F32, tag="bank", name=name)

        def side_bank(name):
            return side_banks.tile([P, BANK], F32, tag="side_bank", name=name)

        def chunk(jc):
            return slice(jc * BANK, (jc + 1) * BANK)

        def half(side):
            return slice(side * (N // 2), (side + 1) * (N // 2))

        def repeated(column):
            return column.to_broadcast([P, P])

        def x_block(b, kb):
            first = (b % UB_PER_PANEL) * P
            return x_panels[b // UB_PER_PANEL][:, kb, first : first + P]

        def project(h_ps, b, w_part):
            for kb in range(KB):
                nc.tensor.matmul(h_ps, lhsT=x_block(b, kb), rhs=w_part[:, kb, :], start=(kb == 0), stop=(kb == KB - 1))

        def scaled(out_rows, h_ps, b):
            nc.scalar.activation(out=out_rows, in_=h_ps, func=ACT.Copy, scale=factor[:, b : b + 1])

        def load_window(cb):
            window = windows.tile([P, SLOTS], F32, name="window")
            nc.sync.dma_start(window[:], base[cb * P : (cb + 1) * P, :])
            return window

        offsets = held.tile([P, N // 16], U16, name="offsets")
        h_first = held.tile([P, UB, P + 2], BF16, name="h_first")
        h_rest = [held.tile([P, REST], BF16, name=f"h_rest{b}") for b in range(UB)]
        w_sb = held.tile([P, KB, C], BF16, name="w_sb")
        x_panels = [held.tile([P, KB, BANK], BF16, name=f"x_panel{jc}") for jc in range(JC)]
        factor = held.tile([P, UB], F32, name="factor")
        t = [held.tile([P, N], BF16, name=f"t{b}") for b in range(UB)]
        inv_cols = held.tile([P, JB], F32, name="inv_cols")
        inv_sum = held.tile([P, N], F32, name="inv_sum")
        identity_f32 = held.tile([P, P], F32, name="identity_f32")
        make_identity(nc, identity_f32[:])

        with (
            tc.tile_pool(name="early", bufs=1) as early,
            tc.tile_pool(name="scratch", bufs=2) as scratch,
            tc.tile_pool(name="adjacency", bufs=8) as adjacency,
        ):
            nc.sync.dma_start(w_sb[:], w.rearrange("(kb p) c -> p kb c", p=P))

            def as_rows(vector, name):
                rows = early.tile([P, C], BF16, name=name)
                nc.scalar.dma_start(rows[:], vector.rearrange("c one -> (c one)").partition_broadcast(P))
                return rows

            attn_dst_rows = as_rows(attn_dst, "attn_dst_rows")
            attn_src_rows = as_rows(attn_src, "attn_src_rows")
            for jc in range(JC):
                nc.sync.dma_start(x_panels[jc][:], x[:, chunk(jc)].rearrange("(kb p) u -> p kb u", p=P))
            nc.sync.dma_start(offsets[:], offs)

            def times_w(rows, rounded, name):
                summed = early.tile([P, KB], F32, name=f"{name}_f32")
                for kb in range(KB):
                    products = scratch.tile([P, C], F32, name="products")
                    nc.vector.scalar_tensor_tensor(
                        out=products[:], in0=w_sb[:, kb, :], scalar=1.0, in1=rows[:],
                        op0=ALU.mult, op1=ALU.mult, accum_out=summed[:, kb : kb + 1],
                    )
                nc.vector.tensor_copy(rounded, summed[:])

            w_attn_dst = early.tile([P, KB], BF16, name="w_attn_dst")
            times_w(attn_dst_rows, w_attn_dst[:], "w_attn_dst")
            w_first = early.tile([P, KB, P + 2], BF16, name="w_first")
            nc.scalar.copy(w_first[:, :, 0:P], w_sb[:, :, 0:P])
            times_w(attn_src_rows, w_first[:, :, P], "w_attn_src")

            bias_steep = early.tile([P, 1], F32, name="bias_steep")
            bias_flat = early.tile([P, 1], F32, name="bias_flat")
            receiver_rows = early.tile([P, N], BF16, name="receiver_rows")
            for jc in range(JC):
                a_dst_ps = bank(f"a_dst_ps{jc}")
                for kb in range(KB):
                    nc.tensor.matmul(
                        a_dst_ps[:], lhsT=repeated(w_attn_dst[:, kb : kb + 1]), rhs=x_panels[jc][:, kb, :],
                        start=(kb == 0), stop=(kb == KB - 1),
                    )
                if jc == 0:
                    nc.scalar.mul(bias_steep[:], a_dst_ps[:, 0:1], 1.0 - SLOPE)
                    nc.scalar.mul(bias_flat[:], a_dst_ps[:, 0:1], SLOPE)
                nc.scalar.activation(
                    out=receiver_rows[:, chunk(jc)], in_=a_dst_ps[:], func=ACT.Exp, bias=bias_steep[:, 0:1],
                    scale=SLOPE - 1.0,
                )

            sender_floor = early.tile([P, UB], F32, name="sender_floor")
            for k in range(SUM_BANKS):
                blocks = slice(k * BLOCKS_PER_BANK, min((k + 1) * BLOCKS_PER_BANK, UB))
                n = blocks.stop - blocks.start
                h_ps = bank(f"h_ps{k}")
                for i in range(n):
                    project(h_ps[:, i * WIDTH : (i + 1) * WIDTH], blocks.start + i, w_first[:, :, 0:WIDTH])
                a_src_cols = h_ps[:, P : n * WIDTH : WIDTH]
                nc.scalar.activation(
                    out=sender_floor[:, blocks], in_=a_src_cols, func=ACT.Exp, bias=bias_steep[:, 0:1], scale=1.0 - SLOPE
                )
                nc.scalar.activation(
                    out=factor[:, blocks], in_=a_src_cols, func=ACT.Exp, bias=bias_flat[:, 0:1], scale=SLOPE
                )
                nc.scalar.activation(
                    out=h_first[:, blocks, P], in_=a_src_cols, func=ACT.Exp, bias=bias_flat[:, 0:1], scale=SLOPE
                )
                for i in range(n):
                    b = blocks.start + i
                    scaled(h_first[:, b, 0:P], h_ps[:, i * WIDTH : i * WIDTH + P], b)

            sum_banks = [bank(f"sum_bank{k}") for k in range(SUM_BANKS)]
            def make_t(b, adj, receivers):
                nc.vector.scalar_tensor_tensor(
                    out=t[b][:, receivers], in0=receiver_rows[:, receivers], scalar=sender_floor[:, b : b + 1],
                    in1=adj[:, receivers], op0=ALU.max, op1=ALU.mult,
                )

            def aggregate_first(b, jbs):
                for jb in jbs:
                    k, seat = divmod(jb, BLOCKS_PER_BANK)
                    last_in_bank = seat == BLOCKS_PER_BANK - 1 or jb == JB - 1
                    nc.tensor.matmul(
                        sum_banks[k][:, seat * WIDTH : (seat + 1) * WIDTH], lhsT=t[b][:, jb * P : (jb + 1) * P],
                        rhs=h_first[:, b, 0:WIDTH], start=(b == 0 and seat == 0), stop=(b == UB - 1 and last_in_bank),
                    )

            last_adj = {}
            for b in range(UB):
                adj = adjacency.tile([P, N], F32, name="adj")
                nc.sync.dma_start(adj[:], adj_t[b * P : (b + 1) * P, :])
                if b < UB - HALVED_BLOCKS:
                    make_t(b, adj, slice(0, N))
                    aggregate_first(b, range(JB))
                else:
                    last_adj[b] = adj
                rest_ps = side_bank(f"rest_ps{b}")
                project(rest_ps[:, 0:REST], b, w_sb[:, :, P:C])
                scaled(h_rest[b][:], rest_ps[:, 0:REST], b)
            for side in range(2):
                for b, adj in last_adj.items():
                    make_t(b, adj, half(side))
                    aggregate_first(b, range(side * JB // 2, (side + 1) * JB // 2))

            loaded = [load_window(0), load_window(1)]

        with (
            tc.tile_pool(name="addends", bufs=2) as addends,
            tc.tile_pool(name="turned", bufs=1) as turned,
        ):

            def finish(cb, exp_v, p, q):
                for part in (half(0), chunk(2), chunk(3)):
                    nc.vector.tensor_scalar(
                        out=q[:, part], in0=exp_v[:, part], scalar1=1.0, scalar2=-1.0,
                        op0=ALU.min, op1=ALU.add,
                    )
                nc.vector.tensor_tensor(loaded[cb][:].indirect(offsets[:]), p[:], q[:], ALU.add)
                nc.sync.dma_start(out[cb * P : (cb + 1) * P, :], loaded[cb][:])
                if cb + 2 < CB:
                    loaded.append(load_window(cb + 2))

            v_turned = turned.tile([P, JB, P], F32, name="v_turned")
            for k in range(SUM_BANKS):
                jbs = range(k * BLOCKS_PER_BANK, min((k + 1) * BLOCKS_PER_BANK, JB))
                n = len(jbs)
                inv = inv_cols[:, jbs[0] : jbs[0] + n]
                nc.vector.reciprocal(inv, sum_banks[k][:, P : n * WIDTH : WIDTH])
                if k % 2 == 0:
                    nc.vector.tensor_tensor(
                        v_turned[:, jbs[0] : jbs[0] + n, :],
                        sum_banks[k][:, 0 : n * WIDTH].rearrange("p (j c) -> p j c", c=WIDTH)[:, :, 0:P],
                        inv.unsqueeze(2).to_broadcast([P, n, P]), ALU.mult,
                    )
                else:
                    for i, jb in enumerate(jbs):
                        nc.scalar.activation(
                            out=v_turned[:, jb, :], in_=sum_banks[k][:, i * WIDTH : i * WIDTH + P], func=ACT.Copy,
                            scale=inv_cols[:, jb : jb + 1],
                        )
            exp_v = addends.tile([P, N], F32, name="exp_v")
            p = addends.tile([P, N], F32, name="p")
            q = addends.tile([P, N], F32, name="v")
            for jc in range(JC):
                v_ps = bank(f"turned_ps{jc}")
                for i in range(JB_PER_BANK):
                    nc.tensor.transpose(v_ps[:, i * P : (i + 1) * P], v_turned[:, jc * JB_PER_BANK + i, :], identity_f32[:])
                nc.scalar.activation(out=exp_v[:, chunk(jc)], in_=v_ps[:], func=ACT.Exp)
                if jc % 2 == 0:
                    nc.scalar.activation(out=p[:, chunk(jc)], in_=v_ps[:], func=ACT.Relu)
                else:
                    nc.vector.tensor_scalar_max(p[:, chunk(jc)], v_ps[:], 0.0)
            finish(0, exp_v, p, q)

            inv_ps = bank("inv_ps")
            nc.tensor.transpose(inv_ps[0:JB, 0:P], inv_cols[:], identity_f32[:])
            inv_rows = turned.tile([P, P], F32, name="inv_rows")
            nc.vector.tensor_copy(inv_rows[0:JB, :], inv_ps[0:JB, 0:P])
            parked = out[C - 1 : C, 0:N]
            nc.sync.dma_start(parked.rearrange("one (jb p) -> (one jb) p", p=P), inv_rows[0:JB, :])
            nc.sync.dma_start(inv_sum[:], parked.rearrange("one j -> (one j)").partition_broadcast(P))

            for cb in range(1, CB):
                v = addends.tile([P, N], F32, name="v")
                exp_v = addends.tile([P, N], F32, name="exp_v")
                p = addends.tile([P, N], F32, name="p")
                q = v
                for jc in range(JC):
                    v_ps = (side_bank if cb == 1 and jc < SIDE_BANKS else bank)(f"v_ps{cb}_{jc}")
                    for b in reversed(range(UB)):
                        nc.tensor.matmul(
                            v_ps[:], lhsT=h_rest[b][:, (cb - 1) * P : cb * P], rhs=t[b][:, chunk(jc)],
                            start=(b == UB - 1), stop=(b == 0),
                        )
                    nc.vector.tensor_tensor(v[:, chunk(jc)], v_ps[:], inv_sum[:, chunk(jc)], ALU.mult)
                    nc.scalar.activation(out=exp_v[:, chunk(jc)], in_=v[:, chunk(jc)], func=ACT.Exp)
                nc.scalar.activation(out=p[:, chunk(0)], in_=v[:, chunk(0)], func=ACT.Relu)
                nc.vector.tensor_scalar_max(p[:, BANK:N], v[:, BANK:N], 0.0)
                finish(cb, exp_v, p, q)
